import numpy as np
import ml_dtypes


def mxq(x, axis, fmt="e4m3"):
    dtype, down = {"e4m3": (ml_dtypes.float8_e4m3fn, 7), "e5m2": (ml_dtypes.float8_e5m2, 14)}[fmt]
    v = np.moveaxis(np.asarray(x, np.float32).astype(ml_dtypes.bfloat16).astype(np.float64), axis, -1)
    blocks = v.reshape(v.shape[:-1] + (-1, 32))
    amax = np.abs(blocks).max(-1, keepdims=True)
    byte = np.maximum(np.where(amax > 0, np.frexp(amax)[1] - 1 + 127, 0) - down, 1)
    scale = np.exp2(byte - 127.0)
    codes = (blocks / scale).astype(np.float32).astype(dtype).astype(np.float64)
    return np.moveaxis((codes * scale).reshape(v.shape), -1, axis)


WIDE = False


def mx_kscale(k):
    if not WIDE:
        return np.ones(k)
    levels = np.array([10, -10, 5, -5, 0])
    a = np.random.permutation(np.resize(levels, k // 512 * 4)).reshape(k // 512, 4)
    idx = np.arange(k)
    return np.exp2(a[idx // 512, idx % 128 // 32])


BF16 = ml_dtypes.bfloat16


def bf(x):
    return np.asarray(x, np.float32).astype(BF16)


def f64(x):
    return np.asarray(x).astype(np.float64)


E2M1 = np.array([0.0, 0.5, 1.0, 1.5, 2.0, 3.0, 4.0, 6.0, -0.0, -0.5, -1.0, -1.5, -2.0, -3.0, -4.0, -6.0])


def pack_weight(w, fmt):
    k, n = w.shape
    w = f64(bf(w)).reshape(k // 32, 32, n)
    amax = np.abs(w).max(1)
    if fmt == "e4m3":
        byte = np.frexp(amax)[1] - 1 + 127 - 7
    else:
        mant, ex = np.frexp(amax / 6.0)
        byte = np.where(mant > 0.5, ex, ex - 1) + 127
    byte = np.clip(np.where(amax > 0, byte, 1), 1, 254)
    scaled = (w * np.exp2(127.0 - byte)[:, None, :]).reshape(k, n).astype(np.float32)
    by_word = np.ascontiguousarray(scaled.reshape(k // 512, 128, 4, n).transpose(0, 1, 3, 2))
    if fmt == "e4m3":
        words = by_word.astype(ml_dtypes.float8_e4m3fn).view(np.uint8)
    else:
        c = by_word.astype(ml_dtypes.float4_e2m1fn).view(np.uint8) & 0xF
        words = c[..., 0::2] | (c[..., 1::2] << 4)
    return np.ascontiguousarray(words), np.ascontiguousarray(byte.astype(np.uint8).reshape(k // 512, 16, n))


def unpack_weight(words, scales, fmt):
    g, p, n, _ = words.shape
    if fmt == "e4m3":
        vals = np.ascontiguousarray(words).view(ml_dtypes.float8_e4m3fn).astype(np.float64)
    else:
        nib = np.empty((g, p, n, 4), np.uint8)
        nib[..., 0::2] = words & 0xF
        nib[..., 1::2] = words >> 4
        vals = E2M1[nib]
    vals = vals * np.repeat(np.exp2(scales.astype(np.float64) - 127.0), 8, axis=1)[..., None]
    return vals.transpose(0, 1, 3, 2).reshape(g * 512, n)


N, CIN, COUT, V, T, S = 1, 512, 128, 32, 128, 16
EPS = 1e-5
KG = S * V


def setup_inputs():
    r = np.random.standard_normal
    c = mx_kscale(CIN)
    g = mx_kscale(KG).reshape(S, V)
    ada_A = bf(r((N, CIN, V, V)) * c[None, :, None, None])
    stack = (r((S, COUT, CIN)) / np.sqrt(CIN) / c).swapaxes(1, 2)
    words, scales = pack_weight(stack.reshape(-1, COUT), "e4m3")
    return {"ada_A": ada_A,
            "ada_w_words": words,
            "ada_w_scales": scales,
            "ada_b": bf(r((S, COUT)) * 0.3),
            "PA": bf(r((S, V, V)) * 2.0 / np.sqrt(KG) * g[:, None, :]),
            "feat": bf(r((S, N, COUT, V, T)) / g[:, None, None, :, None]),
            "bn_gamma": bf(1.0 + 0.1 * r(COUT)),
            "bn_beta": bf(0.3 * r(COUT)),
            "bn_mean": bf(0.3 * r(COUT)),
            "bn_var": bf(np.abs(r(COUT)) + 1.0),
            "res": bf(r((N, COUT, V, T)) * 0.9)}


def reference(ada_A, ada_w_words, ada_w_scales, ada_b, PA, feat, bn_gamma, bn_beta, bn_mean, bn_var, res):
    wq = unpack_weight(ada_w_words, ada_w_scales, "e4m3").reshape(S, CIN, COUT).swapaxes(1, 2).reshape(S * COUT, CIN)
    aq = mxq(f64(ada_A).reshape(N, CIN, V * V), 1, "e4m3")
    adaA = (wq @ aq).reshape(N, S, COUT, V, V).transpose(1, 0, 2, 3, 4) + f64(ada_b)[:, None, :, None, None]
    A_full = adaA * f64(PA)[:, None, None, :, :]
    Ag = A_full.transpose(1, 2, 3, 0, 4).reshape(N, COUT, V, KG)
    Fg = f64(feat).transpose(1, 2, 0, 3, 4).reshape(N, COUT, KG, T)
    y = mxq(Ag, 3, "e4m3") @ mxq(Fg, 2, "e4m3")
    scale = f64(bn_gamma) / np.sqrt(f64(bn_var) + EPS)
    z = (y - f64(bn_mean)[:, None, None]) * scale[:, None, None] + f64(bn_beta)[:, None, None]
    return np.maximum(z + f64(res), 0.0)

@@ -1,0 +1,341 @@
+from contextlib import ExitStack
+
+import concourse.mybir as mybir
+from concourse.masks import make_identity
+
+F32 = mybir.dt.float32
+BF16 = mybir.dt.bfloat16
+U32 = mybir.dt.uint32
+I32 = mybir.dt.int32
+U8 = mybir.dt.uint8
+FP8X4 = mybir.dt.float8_e4m3fn_x4
+ALU = mybir.AluOpType
+ACT = mybir.ActivationFunctionType
+
+P = 128
+PACK = 4
+S = 16
+O = 128
+V = 32
+W = 32
+W8 = W // PACK
+T = 128
+EPS = 1e-5
+
+SLOTS = 4
+GROUPS = O // SLOTS
+BANK_GROUPS = 4
+BANKS = GROUPS // BANK_GROUPS
+SLOT_STEP = P + V
+
+V_ROUND = 8
+ROUNDS = V // V_ROUND
+F_BLOCK = 8
+F_BLOCKS = O // F_BLOCK
+F_AHEAD = 3
+FLIP_FIRST = 2
+FLIP_END = FLIP_FIRST + 2 * ROUNDS
+F_FIRST_TILE = F_BLOCK * FLIP_END
+F_VECTOR = 2
+F_GPSIMD = 4
+
+FLOPS = 2 * S * O * 512 * V * W + 2 * O * V * S * W * T
+
+
+def tile_multiscale_gcn_pa_e_kernel(
+    tc, ada_A, ada_w_words, ada_w_scales, ada_b, PA, feat, bn_gamma, bn_beta, bn_mean, bn_var, res, out
+):
+    nc = tc.nc
+    with ExitStack() as ctx:
+        ctx.enter_context(tc.manual_schedule())
+        keep = ctx.enter_context(tc.tile_pool(name="keep", bufs=1))
+        stage = ctx.enter_context(tc.tile_pool(name="stage", bufs=3))
+
+        ident_bf = keep.tile([P, P], BF16, name="ident_bf")
+        make_identity(nc, ident_bf[:])
+        ident_f32 = keep.tile([P, P], F32, name="ident_f32")
+        make_identity(nc, ident_f32[:])
+
+        masked = [
+            keep.tile([P, BANK_GROUPS, SLOTS * SLOT_STEP], U32, name="masked%d" % i, align_bytes=64)
+            for i in range(2)
+        ]
+        for i in range(2):
+            nc.gpsimd.memset(masked[i][:].bitcast(F32), 0.0)
+
+        f_codes = [keep.tile([P, F_FIRST_TILE * T], U32, name="f_codes0", align_bytes=64)]
+        f_scales = [keep.tile([P, F_FIRST_TILE * T], U8, name="f_scales0", align_bytes=64)]
+        adj_codes = keep.tile([P, O * V], U32, name="adj_codes", align_bytes=64)
+        adj_scales = keep.tile([P, O * V], U8, name="adj_scales", align_bytes=64)
+        adj = keep.tile([P, O, V, PACK], BF16, name="adj", align_bytes=64)
+
+        def feat_words(o, n):
+            which = 0 if o < F_FIRST_TILE else 1
+            first = o - which * F_FIRST_TILE
+            return which, slice(T * first, T * (first + n))
+
+        f_raw = {}
+        f_grp = {}
+
+        def feat_load(fb):
+            f_raw[fb] = stage.tile([P, F_BLOCK, PACK, T], BF16, tag="raw", bufs=F_AHEAD + 1, name="f_raw")
+            for c in range(F_BLOCK):
+                nc.sync.dma_start(
+                    out=f_raw[fb][:, c].rearrange("p j t -> p (j t)"),
+                    in_=feat[:, 0, F_BLOCK * fb + c].rearrange("s (w8 j) t -> s w8 (j t)", j=PACK),
+                )
+
+        def feat_regroup(fb):
+            flipping = FLIP_FIRST <= fb < FLIP_END
+            n_vector = 0 if flipping else F_VECTOR
+            n_gpsimd = F_GPSIMD if flipping else 0
+            f_grp[fb] = stage.tile([P, F_BLOCK, T, PACK], BF16, tag="grp", name="f_grp", align_bytes=64)
+            if n_vector > 0:
+                nc.vector.tensor_copy(
+                    out=f_grp[fb][:, 0:n_vector].rearrange("p c (tc i) j -> p c tc j i", i=4),
+                    in_=f_raw[fb][:, 0:n_vector].rearrange("p c j (tc i) -> p c tc j i", i=4),
+                )
+            if n_gpsimd > 0:
+                nc.gpsimd.tensor_scalar(
+                    out=f_grp[fb][:, 0:n_gpsimd],
+                    in0=f_raw[fb][:, 0:n_gpsimd].rearrange("p c j t -> p c t j"),
+                    scalar1=1.0,
+                    scalar2=0.0,
+                    op0=ALU.mult,
+                    op1=ALU.add,
+                )
+            for c in range(n_vector + n_gpsimd, F_BLOCK):
+                nc.scalar.copy(
+                    out=f_grp[fb][:, c].rearrange("p (tc i) j -> p tc j i", i=4),
+                    in_=f_raw[fb][:, c].rearrange("p j (tc i) -> p tc j i", i=4),
+                )
+
+        def feat_quantise(fb):
+            which, words = feat_words(F_BLOCK * fb, F_BLOCK)
+            nc.vector.quantize_mx(
+                out=f_codes[which][:, words].bitcast(FP8X4),
+                scales=f_scales[which][:, words],
+                in_=f_grp[fb][:].rearrange("p c t j -> p (c t j)"),
+            )
+
+        def feat_step(step):
+            if step + F_AHEAD < F_BLOCKS:
+                feat_load(step + F_AHEAD)
+            if step < F_BLOCKS:
+                feat_regroup(step)
+
+        with tc.tile_pool(name="conv", bufs=1) as conv:
+            x_tiles = {}
+            w_words = conv.tile([P, S, P], U32, name="w_words", align_bytes=64)
+            w_scales = conv.tile([P, S, P], U8, name="w_scales", align_bytes=64)
+            a_codes = conv.tile([P, V * W], U32, name="a_codes", align_bytes=64)
+            a_scales = conv.tile([P, V * W], U8, name="a_scales", align_bytes=64)
+            prm_rows = conv.tile([P, P], BF16, name="prm_rows")
+            pa_rows = conv.tile([P, S * W], BF16, name="pa_rows")
+            prm = keep.tile([P, S + 4], F32, name="prm")
+            pat = keep.tile([P, V, PACK], F32, name="pat")
+            bn = keep.tile([P, 2], F32, name="bn")
+            rstd = keep.tile([P, 1], F32, name="rstd")
+
+            nc.vector.memset(w_scales[:].bitcast(I32), 0)
+            nc.vector.memset(prm_rows[:], 0.0)
+            nc.vector.memset(pa_rows[:], 0.0)
+            nc.scalar.dma_start(out=prm_rows[0:S, :], in_=ada_b)
+            for r, vec in enumerate((bn_gamma, bn_beta, bn_mean, bn_var)):
+                nc.scalar.dma_start(out=prm_rows[S + r : S + r + 1, :], in_=vec.unsqueeze(0))
+            nc.scalar.dma_start(
+                out=pa_rows[0:V, :].rearrange("v (s w) -> v s w", w=W), in_=PA.rearrange("s v w -> v s w")
+            )
+            a_raw = stage.tile([P, PACK, V * W], BF16, tag="raw", bufs=F_AHEAD + 1, name="a_raw")
+            a_view = ada_A.rearrange("n (p i) v w -> p (n i) (v w)", i=PACK)
+            half_cols = V * W // 2
+            nc.sync.dma_start(out=a_raw[:, :, 0:half_cols], in_=a_view[:, :, 0:half_cols])
+            for quad in range(4):
+                nc.sync.dma_start(
+                    out=w_scales[32 * quad : 32 * quad + 4].bitcast(I32),
+                    in_=ada_w_scales[:, 4 * quad : 4 * quad + 4, :].rearrange("g r n -> r g n").bitcast(I32),
+                )
+            nc.sync.dma_start(
+                out=w_words[:].bitcast(I32), in_=ada_w_words.rearrange("g p n t -> p g (n t)").bitcast(I32)
+            )
+            nc.sync.dma_start(out=a_raw[:, :, half_cols : 2 * half_cols], in_=a_view[:, :, half_cols : 2 * half_cols])
+            for fb in range(F_AHEAD):
+                feat_load(fb)
+
+            with tc.psum_pool(name="psum_head", bufs=1) as psum_head:
+                prm_ps = psum_head.tile([P, P], BF16, name="prm_ps")
+                nc.tensor.transpose(prm_ps[:], prm_rows[:], ident_bf[:])
+                nc.vector.tensor_copy(out=prm[:], in_=prm_ps[:, 0 : S + 4])
+                gamma, beta, mean, var = [prm[:, S + r : S + r + 1] for r in range(4)]
+                nc.vector.tensor_scalar_add(out=rstd[:], in0=var, scalar1=EPS)
+                nc.scalar.sqrt(out=rstd[:], in_=rstd[:])
+                pa_ps = psum_head.tile([P, PACK, P], BF16, name="pa_ps")
+                for j in range(PACK):
+                    nc.tensor.transpose(pa_ps[:, j, :], pa_rows[:, j : S * W : PACK], ident_bf[:])
+                nc.vector.tensor_copy(out=pat[:], in_=pa_ps[:, :, 0:V].rearrange("p j v -> p v j"))
+
+            a_grp = stage.tile([P, V, PACK, W8, PACK], BF16, tag="grp", name="a_grp", align_bytes=64)
+            a_src = a_raw[:].rearrange("p i (v w8 j) -> p v j w8 i", w8=W8, j=PACK)
+            nc.vector.tensor_copy(out=a_grp[:, 0 : V // 2], in_=a_src[:, 0 : V // 2])
+            for j in range(PACK):
+                nc.scalar.copy(out=a_grp[:, V // 2 : V, j], in_=a_src[:, V // 2 : V, j])
+            for h in range(2):
+                nc.vector.quantize_mx(
+                    out=a_codes[:, half_cols * h : half_cols * (h + 1)].bitcast(FP8X4),
+                    scales=a_scales[:, half_cols * h : half_cols * (h + 1)],
+                    in_=a_grp[:, V // 2 * h : V // 2 * (h + 1)].rearrange("p v j w8 i -> p (v j w8 i)"),
+                )
+
+            nc.vector.reciprocal(out=rstd[:], in_=rstd[:])
+            nc.vector.tensor_mul(out=bn[:, 0:1], in0=gamma, in1=rstd[:])
+            nc.vector.tensor_mul(out=rstd[:], in0=mean, in1=bn[:, 0:1])
+            nc.vector.tensor_sub(out=bn[:, 1:2], in0=beta, in1=rstd[:])
+
+            with tc.psum_pool(name="psum_conv", bufs=4) as psum_conv, tc.psum_pool(
+                name="psum_flip", bufs=4
+            ) as psum_flip:
+                n_cols = V_ROUND * W
+
+                def conv_half(r, half):
+                    cols = slice(n_cols * r, n_cols * (r + 1))
+                    for s_pair in range(S // 4 * half, S // 4 * (half + 1)):
+                        conv_ps = psum_conv.tile([P, 2, n_cols], F32, name="conv_ps")
+                        for e in range(2):
+                            s = 2 * s_pair + e
+                            nc.tensor.matmul_mx(
+                                out=conv_ps[:, e, :],
+                                lhsT=w_words[:, s, :].bitcast(FP8X4),
+                                lhsT_scale=w_scales[:, s, :],
+                                rhs=a_codes[:, cols].bitcast(FP8X4),
+                                rhs_scale=a_scales[:, cols],
+                                start=True,
+                                stop=True,
+                            )
+                        for e in range(2):
+                            s = 2 * s_pair + e
+                            nc.scalar.activation(
+                                out=x_tiles[r][:, :, s, :],
+                                in_=conv_ps[:, e, :].rearrange("p (c w8) -> p c w8", w8=W8),
+                                func=ACT.Identity,
+                                bias=prm[:, s : s + 1],
+                                scale=1.0,
+                            )
+
+                def flip_half(r, half):
+                    for vr in range(V_ROUND // 2 * half, V_ROUND // 2 * (half + 1)):
+                        v = V_ROUND * r + vr
+                        flip_ps = psum_flip.tile([P, PACK, O], F32, name="flip_ps")
+                        for j in range(PACK):
+                            nc.tensor.transpose(
+                                flip_ps[:, j, :],
+                                x_tiles[r][:, PACK * vr + j, :, :].rearrange("p s w8 -> p (s w8)"),
+                                ident_f32[:],
+                            )
+                        nc.vector.tensor_tensor(
+                            out=adj[:, :, v, :],
+                            in0=flip_ps[:].rearrange("p j o -> p o j"),
+                            in1=pat[:, v, :].unsqueeze(1).to_broadcast([P, O, PACK]),
+                            op=ALU.mult,
+                        )
+
+                for step in range(FLIP_END):
+                    feat_step(step)
+                    if step >= 1:
+                        feat_quantise(step - 1)
+                    if step < 2 * ROUNDS:
+                        r, half = divmod(step, 2)
+                        if half == 0:
+                            x_tiles[r] = conv.tile([P, V_ROUND * PACK, S, W8], F32, tag="x", bufs=2, name="x")
+                        conv_half(r, half)
+                    if step >= FLIP_FIRST:
+                        r, half = divmod(step - FLIP_FIRST, 2)
+                        flip_half(r, half)
+
+        with tc.tile_pool(name="late", bufs=2, reuse_waits="tile") as late, tc.psum_pool(
+            name="psum_graph", bufs=4
+        ) as psum_graph, tc.psum_pool(name="psum_bn", bufs=1) as psum_bn:
+            f_codes.append(late.tile([P, (O - F_FIRST_TILE) * T], U32, bufs=1, name="f_codes1", align_bytes=64))
+            f_scales.append(late.tile([P, (O - F_FIRST_TILE) * T], U8, bufs=1, name="f_scales1", align_bytes=64))
+            res_sb = late.tile([P, GROUPS, T], BF16, bufs=1, name="res_sb")
+            nc.sync.dma_start(out=res_sb[:], in_=res.rearrange("n (g a) v t -> (n a v) g t", a=SLOTS))
+            out_view = out.rearrange("n (g a) v t -> (n a v) g t", a=SLOTS)
+
+            bn_ps = psum_bn.tile([P, 2, P], F32, name="bn_ps")
+            for c in range(2):
+                nc.tensor.transpose(bn_ps[:, c, :], bn[:, c : c + 1].to_broadcast([P, P]), ident_f32[:])
+            bn_slot = keep.tile([P, 2, GROUPS], F32, name="bn_slot")
+            for a in range(SLOTS):
+                rows = slice(V * a, V * a + V)
+                nc.vector.tensor_copy(out=bn_slot[rows], in_=bn_ps[rows, :, a:P:SLOTS])
+
+            graph_ps = {}
+
+            def adj_quantise(c):
+                o_step = 2 * BANK_GROUPS * SLOTS
+                words = slice(V * o_step * c, V * o_step * (c + 1))
+                nc.vector.quantize_mx(
+                    out=adj_codes[:, words].bitcast(FP8X4),
+                    scales=adj_scales[:, words],
+                    in_=adj[:, o_step * c : o_step * (c + 1)].rearrange("p o v j -> p (o v j)"),
+                )
+
+            def graph_start(b):
+                stat = masked[b % 2]
+                bank_words = slice(BANK_GROUPS * P * b, BANK_GROUPS * P * (b + 1))
+                nc.vector.tensor_copy(
+                    out=stat[:].bitcast(I32).rearrange("p g (a c) -> p g a c", c=SLOT_STEP)[:, :, :, 0:V],
+                    in_=adj_codes[:, bank_words].bitcast(I32).rearrange("p (g a v) -> p g a v", a=SLOTS, v=V),
+                )
+                graph_ps[b] = psum_graph.tile([P, BANK_GROUPS, T], F32, name="graph_ps")
+                for gi in range(BANK_GROUPS):
+                    g = BANK_GROUPS * b + gi
+                    for a in range(SLOTS):
+                        which, words = feat_words(SLOTS * g + a, 1)
+                        nc.tensor.matmul_mx(
+                            out=graph_ps[b][:, gi, :],
+                            lhsT=stat[:, gi, P * a : P * (a + 1)].bitcast(FP8X4),
+                            lhsT_scale=adj_scales[:, P * g : P * (g + 1)],
+                            rhs=f_codes[which][:, words].bitcast(FP8X4),
+                            rhs_scale=f_scales[which][:, words],
+                            start=(a == 0),
+                            stop=(a == SLOTS - 1),
+                        )
+
+            def graph_finish(b):
+                scaled = late.tile([P, BANK_GROUPS, T], F32, name="scaled")
+                result = late.tile([P, BANK_GROUPS, T], F32, name="result")
+                for gi in range(BANK_GROUPS):
+                    g = BANK_GROUPS * b + gi
+                    nc.vector.scalar_tensor_tensor(
+                        out=scaled[:, gi, :],
+                        in0=graph_ps[b][:, gi, :],
+                        scalar=bn_slot[:, 0, g : g + 1],
+                        in1=res_sb[:, g, :],
+                        op0=ALU.mult,
+                        op1=ALU.add,
+                    )
+                for gi in range(BANK_GROUPS):
+                    g = BANK_GROUPS * b + gi
+                    nc.scalar.activation(
+                        out=result[:, gi, :],
+                        in_=scaled[:, gi, :],
+                        func=ACT.Relu,
+                        bias=bn_slot[:, 1, g : g + 1],
+                        scale=1.0,
+                    )
+                nc.scalar.dma_start(out=out_view[:, BANK_GROUPS * b : BANK_GROUPS * (b + 1), :], in_=result[:])
+
+            def banks_started(step):
+                return [b for b in range(BANKS) if max(2 * b + 2, FLIP_END + b // 2) == step]
+
+            for step in range(FLIP_END, F_BLOCKS + 2):
+                feat_step(step)
+                if step - 1 < F_BLOCKS:
+                    feat_quantise(step - 1)
+                for b in banks_started(step):
+                    if b % 2 == 0:
+                        adj_quantise(b // 2)
+                for b in banks_started(step - 1):
+                    graph_finish(b)
+                for b in banks_started(step):
+                    graph_start(b)

@@ -36,8 +36,8 @@ F_AHEAD = 3
 FLIP_FIRST = 2
 FLIP_END = FLIP_FIRST + 2 * ROUNDS
 F_FIRST_TILE = F_BLOCK * FLIP_END
+F_PART = F_BLOCK // 2
 F_VECTOR = 2
-F_GPSIMD = 4
 
 FLOPS = 2 * S * O * 512 * V * W + 2 * O * V * S * W * T
 
@@ -60,8 +60,6 @@ def tile_multiscale_gcn_pa_e_kernel(
             keep.tile([P, BANK_GROUPS, SLOTS * SLOT_STEP], U32, name="masked%d" % i, align_bytes=64)
             for i in range(2)
         ]
-        for i in range(2):
-            nc.gpsimd.memset(masked[i][:].bitcast(F32), 0.0)
 
         f_codes = [keep.tile([P, F_FIRST_TILE * T], U32, name="f_codes0", align_bytes=64)]
         f_scales = [keep.tile([P, F_FIRST_TILE * T], U8, name="f_scales0", align_bytes=64)]
@@ -78,49 +76,58 @@ def tile_multiscale_gcn_pa_e_kernel(
         f_grp = {}
 
         def feat_load(fb):
-            f_raw[fb] = stage.tile([P, F_BLOCK, PACK, T], BF16, tag="raw", bufs=F_AHEAD + 1, name="f_raw")
+            f_raw[fb] = stage.tile([P, F_BLOCK, PACK, T], BF16, tag="raw", bufs=F_AHEAD + 1, name="f_raw", align_bytes=64)
             for c in range(F_BLOCK):
                 nc.sync.dma_start(
                     out=f_raw[fb][:, c].rearrange("p j t -> p (j t)"),
                     in_=feat[:, 0, F_BLOCK * fb + c].rearrange("s (w8 j) t -> s w8 (j t)", j=PACK),
                 )
 
+        def regroup_on_scalar(dst, src):
+            nc.scalar.copy(
+                out=dst.rearrange("p (tc i) j -> p tc j i", i=4), in_=src.rearrange("p j (tc i) -> p tc j i", i=4)
+            )
+
         def feat_regroup(fb):
-            flipping = FLIP_FIRST <= fb < FLIP_END
-            n_vector = 0 if flipping else F_VECTOR
-            n_gpsimd = F_GPSIMD if flipping else 0
-            f_grp[fb] = stage.tile([P, F_BLOCK, T, PACK], BF16, tag="grp", name="f_grp", align_bytes=64)
-            if n_vector > 0:
-                nc.vector.tensor_copy(
-                    out=f_grp[fb][:, 0:n_vector].rearrange("p c (tc i) j -> p c tc j i", i=4),
-                    in_=f_raw[fb][:, 0:n_vector].rearrange("p c j (tc i) -> p c tc j i", i=4),
-                )
-            if n_gpsimd > 0:
+            raw = f_raw[fb]
+            part1 = stage.tile([P, F_PART, T, PACK], BF16, tag="grp_scalar", bufs=3, name="part1", align_bytes=64)
+            if fb < FLIP_END:
+                part0 = stage.tile([P, F_PART, T, PACK], BF16, tag="grp_gpsimd", bufs=1, name="part0", align_bytes=64)
                 nc.gpsimd.tensor_scalar(
-                    out=f_grp[fb][:, 0:n_gpsimd],
-                    in0=f_raw[fb][:, 0:n_gpsimd].rearrange("p c j t -> p c t j"),
+                    out=part0[:],
+                    in0=raw[:, 0:F_PART].rearrange("p c j t -> p c t j"),
                     scalar1=1.0,
                     scalar2=0.0,
                     op0=ALU.mult,
                     op1=ALU.add,
                 )
-            for c in range(n_vector + n_gpsimd, F_BLOCK):
-                nc.scalar.copy(
-                    out=f_grp[fb][:, c].rearrange("p (tc i) j -> p tc j i", i=4),
-                    in_=f_raw[fb][:, c].rearrange("p j (tc i) -> p tc j i", i=4),
+            else:
+                part0 = stage.tile([P, F_PART, T, PACK], BF16, tag="grp_vector", bufs=2, name="part0", align_bytes=64)
+                nc.vector.tensor_copy(
+                    out=part0[:, 0:F_VECTOR].rearrange("p c (tc i) j -> p c tc j i", i=4),
+                    in_=raw[:, 0:F_VECTOR].rearrange("p c j (tc i) -> p c tc j i", i=4),
                 )
+            for c in range(F_PART):
+                regroup_on_scalar(part1[:, c], raw[:, F_PART + c])
+            if fb >= FLIP_END:
+                for c in range(F_VECTOR, F_PART):
+                    regroup_on_scalar(part0[:, c], raw[:, c])
+            f_grp[fb] = (part0, part1)
 
         def feat_quantise(fb):
-            which, words = feat_words(F_BLOCK * fb, F_BLOCK)
-            nc.vector.quantize_mx(
-                out=f_codes[which][:, words].bitcast(FP8X4),
-                scales=f_scales[which][:, words],
-                in_=f_grp[fb][:].rearrange("p c t j -> p (c t j)"),
-            )
+            for part in (1, 0):
+                which, words = feat_words(F_BLOCK * fb + F_PART * part, F_PART)
+                nc.vector.quantize_mx(
+                    out=f_codes[which][:, words].bitcast(FP8X4),
+                    scales=f_scales[which][:, words],
+                    in_=f_grp[fb][part][:].rearrange("p c t j -> p (c t j)"),
+                )
 
         def feat_step(step):
             if step + F_AHEAD < F_BLOCKS:
                 feat_load(step + F_AHEAD)
+            if 1 <= step <= F_BLOCKS:
+                feat_quantise(step - 1)
             if step < F_BLOCKS:
                 feat_regroup(step)
 
@@ -140,13 +147,15 @@ def tile_multiscale_gcn_pa_e_kernel(
             nc.vector.memset(w_scales[:].bitcast(I32), 0)
             nc.vector.memset(prm_rows[:], 0.0)
             nc.vector.memset(pa_rows[:], 0.0)
+            for i in range(2):
+                nc.vector.memset(masked[i][:].bitcast(I32), 0)
             nc.scalar.dma_start(out=prm_rows[0:S, :], in_=ada_b)
             for r, vec in enumerate((bn_gamma, bn_beta, bn_mean, bn_var)):
                 nc.scalar.dma_start(out=prm_rows[S + r : S + r + 1, :], in_=vec.unsqueeze(0))
             nc.scalar.dma_start(
                 out=pa_rows[0:V, :].rearrange("v (s w) -> v s w", w=W), in_=PA.rearrange("s v w -> v s w")
             )
-            a_raw = stage.tile([P, PACK, V * W], BF16, tag="raw", bufs=F_AHEAD + 1, name="a_raw")
+            a_raw = stage.tile([P, PACK, V * W], BF16, tag="raw", bufs=F_AHEAD + 1, name="a_raw", align_bytes=64)
             a_view = ada_A.rearrange("n (p i) v w -> p (n i) (v w)", i=PACK)
             half_cols = V * W // 2
             nc.sync.dma_start(out=a_raw[:, :, 0:half_cols], in_=a_view[:, :, 0:half_cols])
@@ -159,8 +168,6 @@ def tile_multiscale_gcn_pa_e_kernel(
                 out=w_words[:].bitcast(I32), in_=ada_w_words.rearrange("g p n t -> p g (n t)").bitcast(I32)
             )
             nc.sync.dma_start(out=a_raw[:, :, half_cols : 2 * half_cols], in_=a_view[:, :, half_cols : 2 * half_cols])
-            for fb in range(F_AHEAD):
-                feat_load(fb)
 
             with tc.psum_pool(name="psum_head", bufs=1) as psum_head:
                 prm_ps = psum_head.tile([P, P], BF16, name="prm_ps")
@@ -174,17 +181,20 @@ def tile_multiscale_gcn_pa_e_kernel(
                     nc.tensor.transpose(pa_ps[:, j, :], pa_rows[:, j : S * W : PACK], ident_bf[:])
                 nc.vector.tensor_copy(out=pat[:], in_=pa_ps[:, :, 0:V].rearrange("p j v -> p v j"))
 
-            a_grp = stage.tile([P, V, PACK, W8, PACK], BF16, tag="grp", name="a_grp", align_bytes=64)
+            a_grp = stage.tile([P, V, PACK, W8, PACK], BF16, tag="raw", bufs=F_AHEAD + 1, name="a_grp", align_bytes=64)
             a_src = a_raw[:].rearrange("p i (v w8 j) -> p v j w8 i", w8=W8, j=PACK)
-            nc.vector.tensor_copy(out=a_grp[:, 0 : V // 2], in_=a_src[:, 0 : V // 2])
-            for j in range(PACK):
-                nc.scalar.copy(out=a_grp[:, V // 2 : V, j], in_=a_src[:, V // 2 : V, j])
             for h in range(2):
+                nc.vector.tensor_copy(
+                    out=a_grp[:, V // 2 * h : V // 2 * (h + 1)], in_=a_src[:, V // 2 * h : V // 2 * (h + 1)]
+                )
                 nc.vector.quantize_mx(
                     out=a_codes[:, half_cols * h : half_cols * (h + 1)].bitcast(FP8X4),
                     scales=a_scales[:, half_cols * h : half_cols * (h + 1)],
                     in_=a_grp[:, V // 2 * h : V // 2 * (h + 1)].rearrange("p v j w8 i -> p (v j w8 i)"),
                 )
+
+            for fb in range(F_AHEAD):
+                feat_load(fb)
 
             nc.vector.reciprocal(out=rstd[:], in_=rstd[:])
             nc.vector.tensor_mul(out=bn[:, 0:1], in0=gamma, in1=rstd[:])
@@ -239,14 +249,12 @@ def tile_multiscale_gcn_pa_e_kernel(
                         )
 
                 for step in range(FLIP_END):
-                    feat_step(step)
-                    if step >= 1:
-                        feat_quantise(step - 1)
                     if step < 2 * ROUNDS:
                         r, half = divmod(step, 2)
                         if half == 0:
                             x_tiles[r] = conv.tile([P, V_ROUND * PACK, S, W8], F32, tag="x", bufs=2, name="x")
                         conv_half(r, half)
+                    feat_step(step)
                     if step >= FLIP_FIRST:
                         r, half = divmod(step - FLIP_FIRST, 2)
                         flip_half(r, half)
@@ -330,8 +338,6 @@ def tile_multiscale_gcn_pa_e_kernel(
 
             for step in range(FLIP_END, F_BLOCKS + 2):
                 feat_step(step)
-                if step - 1 < F_BLOCKS:
-                    feat_quantise(step - 1)
                 for b in banks_started(step):
                     if b % 2 == 0:
                         adj_quantise(b // 2)

@@ -66,6 +66,7 @@ def tile_multiscale_gcn_pa_e_kernel(
         adj_codes = keep.tile([P, O * V], U32, name="adj_codes", align_bytes=64)
         adj_scales = keep.tile([P, O * V], U8, name="adj_scales", align_bytes=64)
         adj = keep.tile([P, O, V, PACK], BF16, name="adj", align_bytes=64)
+        res_sb = keep.tile([P, GROUPS, T], BF16, name="res_sb")
 
         def feat_words(o, n):
             which = 0 if o < F_FIRST_TILE else 1
@@ -74,6 +75,7 @@ def tile_multiscale_gcn_pa_e_kernel(
 
         f_raw = {}
         f_grp = {}
+        late_pool = []
 
         def feat_load(fb):
             f_raw[fb] = stage.tile([P, F_BLOCK, PACK, T], BF16, tag="raw", bufs=F_AHEAD + 1, name="f_raw", align_bytes=64)
@@ -89,6 +91,7 @@ def tile_multiscale_gcn_pa_e_kernel(
             )
 
         def feat_regroup(fb):
+            n_vector = F_PART if fb == F_BLOCKS - 1 else F_VECTOR
             raw = f_raw[fb]
             part1 = stage.tile([P, F_PART, T, PACK], BF16, tag="grp_scalar", bufs=3, name="part1", align_bytes=64)
             if fb < FLIP_END:
@@ -102,15 +105,15 @@ def tile_multiscale_gcn_pa_e_kernel(
                     op1=ALU.add,
                 )
             else:
-                part0 = stage.tile([P, F_PART, T, PACK], BF16, tag="grp_vector", bufs=2, name="part0", align_bytes=64)
+                part0 = late_pool[0].tile([P, F_PART, T, PACK], BF16, tag="grp_vector", name="part0", align_bytes=64)
                 nc.vector.tensor_copy(
-                    out=part0[:, 0:F_VECTOR].rearrange("p c (tc i) j -> p c tc j i", i=4),
-                    in_=raw[:, 0:F_VECTOR].rearrange("p c j (tc i) -> p c tc j i", i=4),
+                    out=part0[:, 0:n_vector].rearrange("p c (tc i) j -> p c tc j i", i=4),
+                    in_=raw[:, 0:n_vector].rearrange("p c j (tc i) -> p c tc j i", i=4),
                 )
             for c in range(F_PART):
                 regroup_on_scalar(part1[:, c], raw[:, F_PART + c])
             if fb >= FLIP_END:
-                for c in range(F_VECTOR, F_PART):
+                for c in range(n_vector, F_PART):
                     regroup_on_scalar(part0[:, c], raw[:, c])
             f_grp[fb] = (part0, part1)
 
@@ -158,15 +161,17 @@ def tile_multiscale_gcn_pa_e_kernel(
             a_raw = stage.tile([P, PACK, V * W], BF16, tag="raw", bufs=F_AHEAD + 1, name="a_raw", align_bytes=64)
             a_view = ada_A.rearrange("n (p i) v w -> p (n i) (v w)", i=PACK)
             half_cols = V * W // 2
+            w_view = ada_w_words.rearrange("g p n t -> p g (n t)").bitcast(I32)
             nc.sync.dma_start(out=a_raw[:, :, 0:half_cols], in_=a_view[:, :, 0:half_cols])
             for quad in range(4):
                 nc.sync.dma_start(
                     out=w_scales[32 * quad : 32 * quad + 4].bitcast(I32),
                     in_=ada_w_scales[:, 4 * quad : 4 * quad + 4, :].rearrange("g r n -> r g n").bitcast(I32),
                 )
-            nc.sync.dma_start(
-                out=w_words[:].bitcast(I32), in_=ada_w_words.rearrange("g p n t -> p g (n t)").bitcast(I32)
-            )
+            for h in range(2):
+                subsets = slice(S // 2 * h, S // 2 * (h + 1))
+                nc.sync.dma_start(out=w_words[:, subsets].bitcast(I32), in_=w_view[:, subsets])
+            feat_load(0)
             nc.sync.dma_start(out=a_raw[:, :, half_cols : 2 * half_cols], in_=a_view[:, :, half_cols : 2 * half_cols])
 
             with tc.psum_pool(name="psum_head", bufs=1) as psum_head:
@@ -193,8 +198,9 @@ def tile_multiscale_gcn_pa_e_kernel(
                     in_=a_grp[:, V // 2 * h : V // 2 * (h + 1)].rearrange("p v j w8 i -> p (v j w8 i)"),
                 )
 
-            for fb in range(F_AHEAD):
+            for fb in range(1, F_AHEAD):
                 feat_load(fb)
+            nc.sync.dma_start(out=res_sb[:], in_=res.rearrange("n (g a) v t -> (n a v) g t", a=SLOTS))
 
             nc.vector.reciprocal(out=rstd[:], in_=rstd[:])
             nc.vector.tensor_mul(out=bn[:, 0:1], in0=gamma, in1=rstd[:])
@@ -262,10 +268,9 @@ def tile_multiscale_gcn_pa_e_kernel(
         with tc.tile_pool(name="late", bufs=2, reuse_waits="tile") as late, tc.psum_pool(
             name="psum_graph", bufs=4
         ) as psum_graph, tc.psum_pool(name="psum_bn", bufs=1) as psum_bn:
+            late_pool.append(late)
             f_codes.append(late.tile([P, (O - F_FIRST_TILE) * T], U32, bufs=1, name="f_codes1", align_bytes=64))
             f_scales.append(late.tile([P, (O - F_FIRST_TILE) * T], U8, bufs=1, name="f_scales1", align_bytes=64))
-            res_sb = late.tile([P, GROUPS, T], BF16, bufs=1, name="res_sb")
-            nc.sync.dma_start(out=res_sb[:], in_=res.rearrange("n (g a) v t -> (n a v) g t", a=SLOTS))
             out_view = out.rearrange("n (g a) v t -> (n a v) g t", a=SLOTS)
 
             bn_ps = psum_bn.tile([P, 2, P], F32, name="bn_ps")
@@ -287,13 +292,15 @@ def tile_multiscale_gcn_pa_e_kernel(
                     in_=adj[:, o_step * c : o_step * (c + 1)].rearrange("p o v j -> p (o v j)"),
                 )
 
-            def graph_start(b):
-                stat = masked[b % 2]
+            def graph_mask(b):
                 bank_words = slice(BANK_GROUPS * P * b, BANK_GROUPS * P * (b + 1))
                 nc.vector.tensor_copy(
-                    out=stat[:].bitcast(I32).rearrange("p g (a c) -> p g a c", c=SLOT_STEP)[:, :, :, 0:V],
+                    out=masked[b % 2][:].bitcast(I32).rearrange("p g (a c) -> p g a c", c=SLOT_STEP)[:, :, :, 0:V],
                     in_=adj_codes[:, bank_words].bitcast(I32).rearrange("p (g a v) -> p g a v", a=SLOTS, v=V),
                 )
+
+            def graph_matmuls(b):
+                stat = masked[b % 2]
                 graph_ps[b] = psum_graph.tile([P, BANK_GROUPS, T], F32, name="graph_ps")
                 for gi in range(BANK_GROUPS):
                     g = BANK_GROUPS * b + gi
@@ -334,14 +341,20 @@ def tile_multiscale_gcn_pa_e_kernel(
                 nc.scalar.dma_start(out=out_view[:, BANK_GROUPS * b : BANK_GROUPS * (b + 1), :], in_=result[:])
 
             def banks_started(step):
-                return [b for b in range(BANKS) if max(2 * b + 2, FLIP_END + b // 2) == step]
+                return [b for b in range(BANKS) if max(2 * b + 2, FLIP_END + max(b - 1, 0)) == step]
 
             for step in range(FLIP_END, F_BLOCKS + 2):
-                feat_step(step)
+                if step + F_AHEAD < F_BLOCKS:
+                    feat_load(step + F_AHEAD)
                 for b in banks_started(step):
                     if b % 2 == 0:
                         adj_quantise(b // 2)
+                    graph_mask(b)
+                if step <= F_BLOCKS:
+                    feat_quantise(step - 1)
+                for b in banks_started(step):
+                    graph_matmuls(b)
+                if step < F_BLOCKS:
+                    feat_regroup(step)
                 for b in banks_started(step - 1):
                     graph_finish(b)
-                for b in banks_started(step):
-                    graph_start(b)

@@ -28,13 +28,14 @@ BANK_GROUPS = 4
 BANKS = GROUPS // BANK_GROUPS
 SLOT_STEP = P + V
 
-V_ROUND = 8
+V_ROUND = 16
 ROUNDS = V // V_ROUND
+S_STEP = 4
+CONV_STEPS = ROUNDS * S // S_STEP
 F_BLOCK = 8
 F_BLOCKS = O // F_BLOCK
 F_AHEAD = 3
-FLIP_FIRST = 2
-FLIP_END = FLIP_FIRST + 2 * ROUNDS
+FLIP_END = 10
 F_FIRST_TILE = F_BLOCK * FLIP_END
 F_PART = F_BLOCK // 2
 F_VECTOR = 2
@@ -66,7 +67,6 @@ def tile_multiscale_gcn_pa_e_kernel(
         adj_codes = keep.tile([P, O * V], U32, name="adj_codes", align_bytes=64)
         adj_scales = keep.tile([P, O * V], U8, name="adj_scales", align_bytes=64)
         adj = keep.tile([P, O, V, PACK], BF16, name="adj", align_bytes=64)
-        res_sb = keep.tile([P, GROUPS, T], BF16, name="res_sb")
 
         def feat_words(o, n):
             which = 0 if o < F_FIRST_TILE else 1
@@ -141,23 +141,17 @@ def tile_multiscale_gcn_pa_e_kernel(
             a_codes = conv.tile([P, V * W], U32, name="a_codes", align_bytes=64)
             a_scales = conv.tile([P, V * W], U8, name="a_scales", align_bytes=64)
             prm_rows = conv.tile([P, P], BF16, name="prm_rows")
-            pa_rows = conv.tile([P, S * W], BF16, name="pa_rows")
             prm = keep.tile([P, S + 4], F32, name="prm")
-            pat = keep.tile([P, V, PACK], F32, name="pat")
             bn = keep.tile([P, 2], F32, name="bn")
             rstd = keep.tile([P, 1], F32, name="rstd")
 
             nc.vector.memset(w_scales[:].bitcast(I32), 0)
             nc.vector.memset(prm_rows[:], 0.0)
-            nc.vector.memset(pa_rows[:], 0.0)
             for i in range(2):
                 nc.vector.memset(masked[i][:].bitcast(I32), 0)
             nc.scalar.dma_start(out=prm_rows[0:S, :], in_=ada_b)
             for r, vec in enumerate((bn_gamma, bn_beta, bn_mean, bn_var)):
                 nc.scalar.dma_start(out=prm_rows[S + r : S + r + 1, :], in_=vec.unsqueeze(0))
-            nc.scalar.dma_start(
-                out=pa_rows[0:V, :].rearrange("v (s w) -> v s w", w=W), in_=PA.rearrange("s v w -> v s w")
-            )
             a_raw = stage.tile([P, PACK, V * W], BF16, tag="raw", bufs=F_AHEAD + 1, name="a_raw", align_bytes=64)
             a_view = ada_A.rearrange("n (p i) v w -> p (n i) (v w)", i=PACK)
             half_cols = V * W // 2
@@ -168,10 +162,24 @@ def tile_multiscale_gcn_pa_e_kernel(
                     out=w_scales[32 * quad : 32 * quad + 4].bitcast(I32),
                     in_=ada_w_scales[:, 4 * quad : 4 * quad + 4, :].rearrange("g r n -> r g n").bitcast(I32),
                 )
-            for h in range(2):
-                subsets = slice(S // 2 * h, S // 2 * (h + 1))
-                nc.sync.dma_start(out=w_words[:, subsets].bitcast(I32), in_=w_view[:, subsets])
+            pab = {}
+
+            def pab_load(step):
+                r, quarter = divmod(step, S // S_STEP)
+                pab[step] = conv.tile([P, S_STEP, V_ROUND * W], BF16, tag="pab", bufs=4, name="pab")
+                nc.sync.dma_start(
+                    out=pab[step][:],
+                    in_=PA[S_STEP * quarter : S_STEP * (quarter + 1), V_ROUND * r : V_ROUND * (r + 1), :]
+                    .rearrange("s v w -> s (v w)")
+                    .partition_broadcast(P),
+                )
+
+            nc.sync.dma_start(out=w_words[:, 0 : S // 2].bitcast(I32), in_=w_view[:, 0 : S // 2])
+            pab_load(0)
             feat_load(0)
+            pab_load(1)
+            nc.sync.dma_start(out=w_words[:, S // 2 : S].bitcast(I32), in_=w_view[:, S // 2 : S])
+            pab_load(2)
             nc.sync.dma_start(out=a_raw[:, :, half_cols : 2 * half_cols], in_=a_view[:, :, half_cols : 2 * half_cols])
 
             with tc.psum_pool(name="psum_head", bufs=1) as psum_head:
@@ -181,26 +189,20 @@ def tile_multiscale_gcn_pa_e_kernel(
                 gamma, beta, mean, var = [prm[:, S + r : S + r + 1] for r in range(4)]
                 nc.vector.tensor_scalar_add(out=rstd[:], in0=var, scalar1=EPS)
                 nc.scalar.sqrt(out=rstd[:], in_=rstd[:])
-                pa_ps = psum_head.tile([P, PACK, P], BF16, name="pa_ps")
-                for j in range(PACK):
-                    nc.tensor.transpose(pa_ps[:, j, :], pa_rows[:, j : S * W : PACK], ident_bf[:])
-                nc.vector.tensor_copy(out=pat[:], in_=pa_ps[:, :, 0:V].rearrange("p j v -> p v j"))
 
-            a_grp = stage.tile([P, V, PACK, W8, PACK], BF16, tag="raw", bufs=F_AHEAD + 1, name="a_grp", align_bytes=64)
-            a_src = a_raw[:].rearrange("p i (v w8 j) -> p v j w8 i", w8=W8, j=PACK)
+            a_grp = stage.tile([P, V * W, PACK], BF16, tag="raw", bufs=F_AHEAD + 1, name="a_grp", align_bytes=64)
             for h in range(2):
-                nc.vector.tensor_copy(
-                    out=a_grp[:, V // 2 * h : V // 2 * (h + 1)], in_=a_src[:, V // 2 * h : V // 2 * (h + 1)]
-                )
+                cols = slice(half_cols * h, half_cols * (h + 1))
+                nc.vector.tensor_copy(out=a_grp[:, cols, :], in_=a_raw[:, :, cols].rearrange("p i c -> p c i"))
                 nc.vector.quantize_mx(
-                    out=a_codes[:, half_cols * h : half_cols * (h + 1)].bitcast(FP8X4),
-                    scales=a_scales[:, half_cols * h : half_cols * (h + 1)],
-                    in_=a_grp[:, V // 2 * h : V // 2 * (h + 1)].rearrange("p v j w8 i -> p (v j w8 i)"),
+                    out=a_codes[:, cols].bitcast(FP8X4),
+                    scales=a_scales[:, cols],
+                    in_=a_grp[:, cols, :].rearrange("p c i -> p (c i)"),
                 )
 
-            for fb in range(1, F_AHEAD):
-                feat_load(fb)
-            nc.sync.dma_start(out=res_sb[:], in_=res.rearrange("n (g a) v t -> (n a v) g t", a=SLOTS))
+            feat_load(1)
+            pab_load(3)
+            feat_load(2)
 
             nc.vector.reciprocal(out=rstd[:], in_=rstd[:])
             nc.vector.tensor_mul(out=bn[:, 0:1], in0=gamma, in1=rstd[:])
@@ -211,59 +213,77 @@ def tile_multiscale_gcn_pa_e_kernel(
                 name="psum_flip", bufs=4
             ) as psum_flip:
                 n_cols = V_ROUND * W
+                conv_ps = {}
+                adj_words = (
+                    adj[:]
+                    .rearrange("p o v j -> p (o v j)")
+                    .bitcast(F32)
+                    .rearrange("p (o v u) -> p o v u", v=V, u=2)
+                )
 
-                def conv_half(r, half):
+                def conv_matmuls(step):
+                    r, quarter = divmod(step, S // S_STEP)
                     cols = slice(n_cols * r, n_cols * (r + 1))
-                    for s_pair in range(S // 4 * half, S // 4 * (half + 1)):
-                        conv_ps = psum_conv.tile([P, 2, n_cols], F32, name="conv_ps")
-                        for e in range(2):
-                            s = 2 * s_pair + e
-                            nc.tensor.matmul_mx(
-                                out=conv_ps[:, e, :],
-                                lhsT=w_words[:, s, :].bitcast(FP8X4),
-                                lhsT_scale=w_scales[:, s, :],
-                                rhs=a_codes[:, cols].bitcast(FP8X4),
-                                rhs_scale=a_scales[:, cols],
-                                start=True,
-                                stop=True,
-                            )
-                        for e in range(2):
-                            s = 2 * s_pair + e
-                            nc.scalar.activation(
-                                out=x_tiles[r][:, :, s, :],
-                                in_=conv_ps[:, e, :].rearrange("p (c w8) -> p c w8", w8=W8),
-                                func=ACT.Identity,
-                                bias=prm[:, s : s + 1],
-                                scale=1.0,
-                            )
-
-                def flip_half(r, half):
-                    for vr in range(V_ROUND // 2 * half, V_ROUND // 2 * (half + 1)):
-                        v = V_ROUND * r + vr
-                        flip_ps = psum_flip.tile([P, PACK, O], F32, name="flip_ps")
-                        for j in range(PACK):
-                            nc.tensor.transpose(
-                                flip_ps[:, j, :],
-                                x_tiles[r][:, PACK * vr + j, :, :].rearrange("p s w8 -> p (s w8)"),
-                                ident_f32[:],
-                            )
-                        nc.vector.tensor_tensor(
-                            out=adj[:, :, v, :],
-                            in0=flip_ps[:].rearrange("p j o -> p o j"),
-                            in1=pat[:, v, :].unsqueeze(1).to_broadcast([P, O, PACK]),
-                            op=ALU.mult,
+                    for s in range(S_STEP * quarter, S_STEP * (quarter + 1)):
+                        conv_ps[s] = psum_conv.tile([P, n_cols], F32, name="conv_ps")
+                        nc.tensor.matmul_mx(
+                            out=conv_ps[s][:],
+                            lhsT=w_words[:, s, :].bitcast(FP8X4),
+                            lhsT_scale=w_scales[:, s, :],
+                            rhs=a_codes[:, cols].bitcast(FP8X4),
+                            rhs_scale=a_scales[:, cols],
+                            start=True,
+                            stop=True,
                         )
 
+                def conv_finish(step):
+                    r, quarter = divmod(step, S // S_STEP)
+                    for i in range(S_STEP):
+                        s = S_STEP * quarter + i
+                        nc.vector.scalar_tensor_tensor(
+                            out=x_tiles[r][:, :, s, :],
+                            in0=conv_ps[s][:].rearrange("p (v w) -> p v w", w=W),
+                            scalar=prm[:, s : s + 1],
+                            in1=pab[step][:, i, :].rearrange("p (v w) -> p v w", w=W),
+                            op0=ALU.add,
+                            op1=ALU.mult,
+                        )
+
+                def flip_pair(pair):
+                    r, v_local = divmod(2 * pair, V_ROUND)
+                    flip_ps = psum_flip.tile([P, 2, 2, O], F32, name="flip_ps")
+                    for dv in range(2):
+                        for u in range(2):
+                            nc.tensor.transpose(
+                                flip_ps[:, dv, u, :],
+                                x_tiles[r][:, v_local + dv].rearrange("p s w -> p (s w)").bitcast(F32)[:, u : S * W // 2 : 2],
+                                ident_f32[:],
+                            )
+                    nc.scalar.copy(
+                        out=adj_words[:, :, 2 * pair : 2 * pair + 2, :], in_=flip_ps[:].rearrange("p v u o -> p o v u")
+                    )
+
+                def pairs_of_step(step):
+                    if 4 <= step < 8:
+                        return range(2 * (step - 4), 2 * (step - 3))
+                    if step >= 8:
+                        return range(8 + 4 * (step - 8), 8 + 4 * (step - 7))
+                    return range(0)
+
                 for step in range(FLIP_END):
-                    if step < 2 * ROUNDS:
-                        r, half = divmod(step, 2)
-                        if half == 0:
-                            x_tiles[r] = conv.tile([P, V_ROUND * PACK, S, W8], F32, tag="x", bufs=2, name="x")
-                        conv_half(r, half)
+                    if step < CONV_STEPS:
+                        if step % (S // S_STEP) == 0:
+                            x_tiles[step // (S // S_STEP)] = conv.tile(
+                                [P, V_ROUND, S, W], BF16, tag="x", bufs=2, name="x"
+                            )
+                        conv_matmuls(step)
+                        if 1 <= step and step + 3 < CONV_STEPS:
+                            pab_load(step + 3)
                     feat_step(step)
-                    if step >= FLIP_FIRST:
-                        r, half = divmod(step - FLIP_FIRST, 2)
-                        flip_half(r, half)
+                    if step < CONV_STEPS:
+                        conv_finish(step)
+                    for pair in pairs_of_step(step):
+                        flip_pair(pair)
 
         with tc.tile_pool(name="late", bufs=2, reuse_waits="tile") as late, tc.psum_pool(
             name="psum_graph", bufs=4
@@ -272,6 +292,8 @@ def tile_multiscale_gcn_pa_e_kernel(
             f_codes.append(late.tile([P, (O - F_FIRST_TILE) * T], U32, bufs=1, name="f_codes1", align_bytes=64))
             f_scales.append(late.tile([P, (O - F_FIRST_TILE) * T], U8, bufs=1, name="f_scales1", align_bytes=64))
             out_view = out.rearrange("n (g a) v t -> (n a v) g t", a=SLOTS)
+            res_sb = late.tile([P, GROUPS, T], BF16, bufs=1, name="res_sb")
+            nc.sync.dma_start(out=res_sb[:], in_=res.rearrange("n (g a) v t -> (n a v) g t", a=SLOTS))
 
             bn_ps = psum_bn.tile([P, 2, P], F32, name="bn_ps")
             for c in range(2):

@@ -141,14 +141,15 @@ def tile_multiscale_gcn_pa_e_kernel(
             a_codes = conv.tile([P, V * W], U32, name="a_codes", align_bytes=64)
             a_scales = conv.tile([P, V * W], U8, name="a_scales", align_bytes=64)
             prm_rows = conv.tile([P, P], BF16, name="prm_rows")
+            pa_rows = conv.tile([P, 2 * P], BF16, name="pa_rows")
+            pa_cols = conv.tile([P, P // 2], F32, name="pa_cols")
             prm = keep.tile([P, S + 4], F32, name="prm")
             bn = keep.tile([P, 2], F32, name="bn")
             rstd = keep.tile([P, 1], F32, name="rstd")
 
             nc.vector.memset(w_scales[:].bitcast(I32), 0)
             nc.vector.memset(prm_rows[:], 0.0)
-            for i in range(2):
-                nc.vector.memset(masked[i][:].bitcast(I32), 0)
+            nc.vector.memset(pa_rows[P // 2 : P, :], 0.0)
             nc.scalar.dma_start(out=prm_rows[0:S, :], in_=ada_b)
             for r, vec in enumerate((bn_gamma, bn_beta, bn_mean, bn_var)):
                 nc.scalar.dma_start(out=prm_rows[S + r : S + r + 1, :], in_=vec.unsqueeze(0))
@@ -156,30 +157,16 @@ def tile_multiscale_gcn_pa_e_kernel(
             a_view = ada_A.rearrange("n (p i) v w -> p (n i) (v w)", i=PACK)
             half_cols = V * W // 2
             w_view = ada_w_words.rearrange("g p n t -> p g (n t)").bitcast(I32)
+            nc.sync.dma_start(out=pa_rows[0 : P // 2, :], in_=PA.rearrange("s (vh vl) w -> (s vh) (vl w)", vl=8))
             nc.sync.dma_start(out=a_raw[:, :, 0:half_cols], in_=a_view[:, :, 0:half_cols])
             for quad in range(4):
                 nc.sync.dma_start(
                     out=w_scales[32 * quad : 32 * quad + 4].bitcast(I32),
                     in_=ada_w_scales[:, 4 * quad : 4 * quad + 4, :].rearrange("g r n -> r g n").bitcast(I32),
                 )
-            pab = {}
-
-            def pab_load(step):
-                r, quarter = divmod(step, S // S_STEP)
-                pab[step] = conv.tile([P, S_STEP, V_ROUND * W], BF16, tag="pab", bufs=4, name="pab")
-                nc.sync.dma_start(
-                    out=pab[step][:],
-                    in_=PA[S_STEP * quarter : S_STEP * (quarter + 1), V_ROUND * r : V_ROUND * (r + 1), :]
-                    .rearrange("s v w -> s (v w)")
-                    .partition_broadcast(P),
-                )
-
             nc.sync.dma_start(out=w_words[:, 0 : S // 2].bitcast(I32), in_=w_view[:, 0 : S // 2])
-            pab_load(0)
             feat_load(0)
-            pab_load(1)
             nc.sync.dma_start(out=w_words[:, S // 2 : S].bitcast(I32), in_=w_view[:, S // 2 : S])
-            pab_load(2)
             nc.sync.dma_start(out=a_raw[:, :, half_cols : 2 * half_cols], in_=a_view[:, :, half_cols : 2 * half_cols])
 
             with tc.psum_pool(name="psum_head", bufs=1) as psum_head:
@@ -189,6 +176,9 @@ def tile_multiscale_gcn_pa_e_kernel(
                 gamma, beta, mean, var = [prm[:, S + r : S + r + 1] for r in range(4)]
                 nc.vector.tensor_scalar_add(out=rstd[:], in0=var, scalar1=EPS)
                 nc.scalar.sqrt(out=rstd[:], in_=rstd[:])
+                pa_ps = psum_head.tile([P, P], F32, name="pa_ps")
+                nc.tensor.transpose(pa_ps[:], pa_rows[:].bitcast(F32), ident_f32[:])
+                nc.vector.tensor_copy(out=pa_cols[:], in_=pa_ps[:, 0 : P // 2])
 
             a_grp = stage.tile([P, V * W, PACK], BF16, tag="raw", bufs=F_AHEAD + 1, name="a_grp", align_bytes=64)
             for h in range(2):
@@ -201,7 +191,6 @@ def tile_multiscale_gcn_pa_e_kernel(
                 )
 
             feat_load(1)
-            pab_load(3)
             feat_load(2)
 
             nc.vector.reciprocal(out=rstd[:], in_=rstd[:])
@@ -210,10 +199,30 @@ def tile_multiscale_gcn_pa_e_kernel(
             nc.vector.tensor_sub(out=bn[:, 1:2], in0=beta, in1=rstd[:])
 
             with tc.psum_pool(name="psum_conv", bufs=4) as psum_conv, tc.psum_pool(
-                name="psum_flip", bufs=4
-            ) as psum_flip:
+                name="psum_flip", bufs=2
+            ) as psum_flip, tc.psum_pool(name="psum_pab", bufs=2) as psum_pab:
                 n_cols = V_ROUND * W
                 conv_ps = {}
+                pab = {}
+
+                def pab_make(step):
+                    r, quarter = divmod(step, S // S_STEP)
+                    pab[step] = conv.tile([P, S_STEP, n_cols], BF16, tag="pab", bufs=4, name="pab")
+                    pab_words = pab[step][:].rearrange("p s c -> p (s c)").bitcast(F32)
+                    for half in range(2):
+                        pab_ps = psum_pab.tile([P, 4, P], F32, name="pab_ps")
+                        for k in range(4):
+                            c = 4 * (S_STEP * quarter + 2 * half + k // 2) + 2 * r + k % 2
+                            nc.tensor.transpose(
+                                pab_ps[:, k, :], pa_cols[:, c : c + 1].to_broadcast([P, P]), ident_f32[:]
+                            )
+                        nc.scalar.copy(
+                            out=pab_words[:, 4 * P * half : 4 * P * (half + 1)],
+                            in_=pab_ps[:].rearrange("p k n -> p (k n)"),
+                        )
+
+                for step in range(4):
+                    pab_make(step)
                 adj_words = (
                     adj[:]
                     .rearrange("p o v j -> p (o v j)")
@@ -278,10 +287,12 @@ def tile_multiscale_gcn_pa_e_kernel(
                             )
                         conv_matmuls(step)
                         if 1 <= step and step + 3 < CONV_STEPS:
-                            pab_load(step + 3)
+                            pab_make(step + 3)
                     feat_step(step)
                     if step < CONV_STEPS:
                         conv_finish(step)
+                    else:
+                        nc.vector.memset(masked[step - CONV_STEPS][:].bitcast(I32), 0)
                     for pair in pairs_of_step(step):
                         flip_pair(pair)
 

@@ -90,6 +90,21 @@ def tile_multiscale_gcn_pa_e_kernel(
                 out=dst.rearrange("p (tc i) j -> p tc j i", i=4), in_=src.rearrange("p j (tc i) -> p tc j i", i=4)
             )
 
+        f_turn = {}
+
+        def feat_turn(fb):
+            f_turn[fb] = late_pool[1].tile([P, T * PACK], F32, name="turn_ps")
+            for i in range(2):
+                nc.tensor.matmul(
+                    out=f_turn[fb][:, T * PACK // 2 * i : T * PACK // 2 * (i + 1)]
+                    .bitcast(BF16)
+                    .rearrange("p (t j) -> p t j", j=PACK),
+                    lhsT=ident_bf[:],
+                    rhs=f_raw[fb][:, F_VECTOR + i].rearrange("p j t -> p t j"),
+                    start=True,
+                    stop=True,
+                )
+
         def feat_regroup(fb):
             n_vector = F_PART if fb == F_BLOCKS - 1 else F_VECTOR
             raw = f_raw[fb]
@@ -112,9 +127,10 @@ def tile_multiscale_gcn_pa_e_kernel(
                 )
             for c in range(F_PART):
                 regroup_on_scalar(part1[:, c], raw[:, F_PART + c])
-            if fb >= FLIP_END:
-                for c in range(n_vector, F_PART):
-                    regroup_on_scalar(part0[:, c], raw[:, c])
+            if fb >= FLIP_END and n_vector < F_PART:
+                nc.scalar.copy(
+                    out=part0[:, n_vector:F_PART].rearrange("p c t j -> p (c t j)").bitcast(F32), in_=f_turn[fb][:]
+                )
             f_grp[fb] = (part0, part1)
 
         def feat_quantise(fb):
@@ -147,18 +163,22 @@ def tile_multiscale_gcn_pa_e_kernel(
             bn = keep.tile([P, 2], F32, name="bn")
             rstd = keep.tile([P, 1], F32, name="rstd")
 
-            nc.vector.memset(w_scales[:].bitcast(I32), 0)
+            warm = keep.tile([P, 1], F32, name="warm")
             nc.vector.memset(prm_rows[:], 0.0)
+            nc.vector.memset(rstd[:], 1.0)
+            nc.vector.memset(w_scales[:].bitcast(I32), 0)
             nc.vector.memset(pa_rows[P // 2 : P, :], 0.0)
             nc.scalar.dma_start(out=prm_rows[0:S, :], in_=ada_b)
             for r, vec in enumerate((bn_gamma, bn_beta, bn_mean, bn_var)):
                 nc.scalar.dma_start(out=prm_rows[S + r : S + r + 1, :], in_=vec.unsqueeze(0))
+            nc.scalar.sqrt(out=warm[:], in_=rstd[:])
             a_raw = stage.tile([P, PACK, V * W], BF16, tag="raw", bufs=F_AHEAD + 1, name="a_raw", align_bytes=64)
             a_view = ada_A.rearrange("n (p i) v w -> p (n i) (v w)", i=PACK)
             half_cols = V * W // 2
             w_view = ada_w_words.rearrange("g p n t -> p g (n t)").bitcast(I32)
-            nc.sync.dma_start(out=pa_rows[0 : P // 2, :], in_=PA.rearrange("s (vh vl) w -> (s vh) (vl w)", vl=8))
             nc.sync.dma_start(out=a_raw[:, :, 0:half_cols], in_=a_view[:, :, 0:half_cols])
+            nc.sync.dma_start(out=pa_rows[0 : P // 2, :], in_=PA.rearrange("s (vh vl) w -> (s vh) (vl w)", vl=8))
+            nc.sync.dma_start(out=a_raw[:, :, half_cols : 2 * half_cols], in_=a_view[:, :, half_cols : 2 * half_cols])
             for quad in range(4):
                 nc.sync.dma_start(
                     out=w_scales[32 * quad : 32 * quad + 4].bitcast(I32),
@@ -167,36 +187,27 @@ def tile_multiscale_gcn_pa_e_kernel(
             nc.sync.dma_start(out=w_words[:, 0 : S // 2].bitcast(I32), in_=w_view[:, 0 : S // 2])
             feat_load(0)
             nc.sync.dma_start(out=w_words[:, S // 2 : S].bitcast(I32), in_=w_view[:, S // 2 : S])
-            nc.sync.dma_start(out=a_raw[:, :, half_cols : 2 * half_cols], in_=a_view[:, :, half_cols : 2 * half_cols])
+            feat_load(1)
+            feat_load(2)
+            nc.vector.memset(masked[0][:].bitcast(I32), 0)
 
-            with tc.psum_pool(name="psum_head", bufs=1) as psum_head:
-                prm_ps = psum_head.tile([P, P], BF16, name="prm_ps")
-                nc.tensor.transpose(prm_ps[:], prm_rows[:], ident_bf[:])
-                nc.vector.tensor_copy(out=prm[:], in_=prm_ps[:, 0 : S + 4])
-                gamma, beta, mean, var = [prm[:, S + r : S + r + 1] for r in range(4)]
-                nc.vector.tensor_scalar_add(out=rstd[:], in0=var, scalar1=EPS)
-                nc.scalar.sqrt(out=rstd[:], in_=rstd[:])
-                pa_ps = psum_head.tile([P, P], F32, name="pa_ps")
-                nc.tensor.transpose(pa_ps[:], pa_rows[:].bitcast(F32), ident_f32[:])
-                nc.vector.tensor_copy(out=pa_cols[:], in_=pa_ps[:, 0 : P // 2])
+            a_grp = {}
 
-            a_grp = stage.tile([P, V * W, PACK], BF16, tag="raw", bufs=F_AHEAD + 1, name="a_grp", align_bytes=64)
-            for h in range(2):
+            def a_regroup(engine_copy, h):
+                a_grp[h] = stage.tile([P, half_cols, PACK], BF16, tag="grp_scalar", bufs=3, name="a_grp", align_bytes=64)
+                engine_copy(
+                    out=a_grp[h][:], in_=a_raw[:, :, half_cols * h : half_cols * (h + 1)].rearrange("p i c -> p c i")
+                )
+
+            def a_quantise(h):
                 cols = slice(half_cols * h, half_cols * (h + 1))
-                nc.vector.tensor_copy(out=a_grp[:, cols, :], in_=a_raw[:, :, cols].rearrange("p i c -> p c i"))
                 nc.vector.quantize_mx(
                     out=a_codes[:, cols].bitcast(FP8X4),
                     scales=a_scales[:, cols],
-                    in_=a_grp[:, cols, :].rearrange("p c i -> p (c i)"),
+                    in_=a_grp[h][:].rearrange("p c i -> p (c i)"),
                 )
 
-            feat_load(1)
-            feat_load(2)
-
-            nc.vector.reciprocal(out=rstd[:], in_=rstd[:])
-            nc.vector.tensor_mul(out=bn[:, 0:1], in0=gamma, in1=rstd[:])
-            nc.vector.tensor_mul(out=rstd[:], in0=mean, in1=bn[:, 0:1])
-            nc.vector.tensor_sub(out=bn[:, 1:2], in0=beta, in1=rstd[:])
+            gamma, beta, mean, var = [prm[:, S + r : S + r + 1] for r in range(4)]
 
             with tc.psum_pool(name="psum_conv", bufs=4) as psum_conv, tc.psum_pool(
                 name="psum_flip", bufs=2
@@ -221,8 +232,21 @@ def tile_multiscale_gcn_pa_e_kernel(
                             in_=pab_ps[:].rearrange("p k n -> p (k n)"),
                         )
 
-                for step in range(4):
+                pa_ps = psum_flip.tile([P, P], F32, tag="flip_ps", name="pa_ps")
+                nc.tensor.transpose(pa_ps[:], pa_rows[:].bitcast(F32), ident_f32[:])
+                nc.vector.tensor_copy(out=pa_cols[:], in_=pa_ps[:, 0 : P // 2])
+                pab_make(0)
+                a_regroup(nc.vector.tensor_copy, 0)
+                a_quantise(0)
+                prm_ps = psum_flip.tile([P, P], BF16, tag="flip_ps", name="prm_ps")
+                nc.tensor.transpose(prm_ps[:], prm_rows[:], ident_bf[:])
+                nc.vector.tensor_copy(out=prm[:], in_=prm_ps[:, 0 : S + 4])
+                nc.vector.tensor_scalar_add(out=rstd[:], in0=var, scalar1=EPS)
+                nc.scalar.sqrt(out=rstd[:], in_=rstd[:])
+                for step in range(1, 4):
                     pab_make(step)
+                a_regroup(nc.vector.tensor_copy, 1)
+                a_quantise(1)
                 adj_words = (
                     adj[:]
                     .rearrange("p o v j -> p (o v j)")
@@ -258,7 +282,7 @@ def tile_multiscale_gcn_pa_e_kernel(
                             op1=ALU.mult,
                         )
 
-                def flip_pair(pair):
+                def flip_pair(pair, engine_copy):
                     r, v_local = divmod(2 * pair, V_ROUND)
                     flip_ps = psum_flip.tile([P, 2, 2, O], F32, name="flip_ps")
                     for dv in range(2):
@@ -268,7 +292,7 @@ def tile_multiscale_gcn_pa_e_kernel(
                                 x_tiles[r][:, v_local + dv].rearrange("p s w -> p (s w)").bitcast(F32)[:, u : S * W // 2 : 2],
                                 ident_f32[:],
                             )
-                    nc.scalar.copy(
+                    engine_copy(
                         out=adj_words[:, :, 2 * pair : 2 * pair + 2, :], in_=flip_ps[:].rearrange("p v u o -> p o v u")
                     )
 
@@ -291,15 +315,23 @@ def tile_multiscale_gcn_pa_e_kernel(
                     feat_step(step)
                     if step < CONV_STEPS:
                         conv_finish(step)
-                    else:
-                        nc.vector.memset(masked[step - CONV_STEPS][:].bitcast(I32), 0)
-                    for pair in pairs_of_step(step):
-                        flip_pair(pair)
+                    if step == CONV_STEPS:
+                        nc.vector.memset(masked[1][:].bitcast(I32), 0)
+                        nc.vector.reciprocal(out=rstd[:], in_=rstd[:])
+                        nc.vector.tensor_mul(out=bn[:, 0:1], in0=gamma, in1=rstd[:])
+                        nc.vector.tensor_mul(out=rstd[:], in0=mean, in1=bn[:, 0:1])
+                        nc.vector.tensor_sub(out=bn[:, 1:2], in0=beta, in1=rstd[:])
+                    n_vector = max(0, step - CONV_STEPS + 1)
+                    for i, pair in enumerate(pairs_of_step(step)):
+                        flip_pair(pair, nc.vector.tensor_copy if i >= 4 - n_vector else nc.scalar.copy)
 
         with tc.tile_pool(name="late", bufs=2, reuse_waits="tile") as late, tc.psum_pool(
             name="psum_graph", bufs=4
-        ) as psum_graph, tc.psum_pool(name="psum_bn", bufs=1) as psum_bn:
+        ) as psum_graph, tc.psum_pool(name="psum_bn", bufs=1) as psum_bn, tc.psum_pool(
+            name="psum_turn", bufs=2
+        ) as psum_turn:
             late_pool.append(late)
+            late_pool.append(psum_turn)
             f_codes.append(late.tile([P, (O - F_FIRST_TILE) * T], U32, bufs=1, name="f_codes1", align_bytes=64))
             f_scales.append(late.tile([P, (O - F_FIRST_TILE) * T], U8, bufs=1, name="f_scales1", align_bytes=64))
             out_view = out.rearrange("n (g a) v t -> (n a v) g t", a=SLOTS)
@@ -379,6 +411,8 @@ def tile_multiscale_gcn_pa_e_kernel(
             for step in range(FLIP_END, F_BLOCKS + 2):
                 if step + F_AHEAD < F_BLOCKS:
                     feat_load(step + F_AHEAD)
+                if step < F_BLOCKS - 1:
+                    feat_turn(step)
                 for b in banks_started(step):
                     if b % 2 == 0:
                         adj_quantise(b // 2)

@@ -26,7 +26,7 @@ SLOTS = 4
 GROUPS = O // SLOTS
 BANK_GROUPS = 4
 BANKS = GROUPS // BANK_GROUPS
-SLOT_STEP = P + V
+GAP = P - V
 
 V_ROUND = 16
 ROUNDS = V // V_ROUND
@@ -58,9 +58,11 @@ def tile_multiscale_gcn_pa_e_kernel(
         make_identity(nc, ident_f32[:])
 
         masked = [
-            keep.tile([P, BANK_GROUPS, SLOTS * SLOT_STEP], U32, name="masked%d" % i, align_bytes=64)
-            for i in range(2)
+            keep.tile([P, BANK_GROUPS * SLOTS, P], U32, name="masked%d" % i, align_bytes=64) for i in range(2)
         ]
+
+        def masked_zero(i):
+            nc.vector.memset(masked[i][:].bitcast(I32)[:, :, 0:GAP], 0)
 
         f_codes = [keep.tile([P, F_FIRST_TILE * T], U32, name="f_codes0", align_bytes=64)]
         f_scales = [keep.tile([P, F_FIRST_TILE * T], U8, name="f_scales0", align_bytes=64)]
@@ -92,15 +94,15 @@ def tile_multiscale_gcn_pa_e_kernel(
 
         f_turn = {}
 
-        def feat_turn(fb):
-            f_turn[fb] = late_pool[1].tile([P, T * PACK], F32, name="turn_ps")
+        def feat_turn(fb, pool, tag, first):
+            f_turn[fb] = pool.tile([P, T * PACK], F32, tag=tag, name="turn_ps")
             for i in range(2):
                 nc.tensor.matmul(
                     out=f_turn[fb][:, T * PACK // 2 * i : T * PACK // 2 * (i + 1)]
                     .bitcast(BF16)
                     .rearrange("p (t j) -> p t j", j=PACK),
                     lhsT=ident_bf[:],
-                    rhs=f_raw[fb][:, F_VECTOR + i].rearrange("p j t -> p t j"),
+                    rhs=f_raw[fb][:, first + i].rearrange("p j t -> p t j"),
                     start=True,
                     stop=True,
                 )
@@ -125,8 +127,13 @@ def tile_multiscale_gcn_pa_e_kernel(
                     out=part0[:, 0:n_vector].rearrange("p c (tc i) j -> p c tc j i", i=4),
                     in_=raw[:, 0:n_vector].rearrange("p c j (tc i) -> p c tc j i", i=4),
                 )
-            for c in range(F_PART):
+            n_scalar = F_PART - 2 if CONV_STEPS <= fb < FLIP_END else F_PART
+            for c in range(n_scalar):
                 regroup_on_scalar(part1[:, c], raw[:, F_PART + c])
+            if n_scalar < F_PART:
+                nc.scalar.copy(
+                    out=part1[:, n_scalar:F_PART].rearrange("p c t j -> p (c t j)").bitcast(F32), in_=f_turn[fb][:]
+                )
             if fb >= FLIP_END and n_vector < F_PART:
                 nc.scalar.copy(
                     out=part0[:, n_vector:F_PART].rearrange("p c t j -> p (c t j)").bitcast(F32), in_=f_turn[fb][:]
@@ -176,20 +183,21 @@ def tile_multiscale_gcn_pa_e_kernel(
             a_view = ada_A.rearrange("n (p i) v w -> p (n i) (v w)", i=PACK)
             half_cols = V * W // 2
             w_view = ada_w_words.rearrange("g p n t -> p g (n t)").bitcast(I32)
-            nc.sync.dma_start(out=a_raw[:, :, 0:half_cols], in_=a_view[:, :, 0:half_cols])
             nc.sync.dma_start(out=pa_rows[0 : P // 2, :], in_=PA.rearrange("s (vh vl) w -> (s vh) (vl w)", vl=8))
-            nc.sync.dma_start(out=a_raw[:, :, half_cols : 2 * half_cols], in_=a_view[:, :, half_cols : 2 * half_cols])
+            nc.sync.dma_start(out=a_raw[:, :, 0:half_cols], in_=a_view[:, :, 0:half_cols])
             for quad in range(4):
                 nc.sync.dma_start(
                     out=w_scales[32 * quad : 32 * quad + 4].bitcast(I32),
                     in_=ada_w_scales[:, 4 * quad : 4 * quad + 4, :].rearrange("g r n -> r g n").bitcast(I32),
                 )
-            nc.sync.dma_start(out=w_words[:, 0 : S // 2].bitcast(I32), in_=w_view[:, 0 : S // 2])
+            nc.sync.dma_start(out=w_words[:, 0:S_STEP].bitcast(I32), in_=w_view[:, 0:S_STEP])
+            nc.sync.dma_start(out=a_raw[:, :, half_cols : 2 * half_cols], in_=a_view[:, :, half_cols : 2 * half_cols])
             feat_load(0)
+            nc.sync.dma_start(out=w_words[:, S_STEP : S // 2].bitcast(I32), in_=w_view[:, S_STEP : S // 2])
             nc.sync.dma_start(out=w_words[:, S // 2 : S].bitcast(I32), in_=w_view[:, S // 2 : S])
             feat_load(1)
             feat_load(2)
-            nc.vector.memset(masked[0][:].bitcast(I32), 0)
+            masked_zero(0)
 
             a_grp = {}
 
@@ -312,11 +320,13 @@ def tile_multiscale_gcn_pa_e_kernel(
                         conv_matmuls(step)
                         if 1 <= step and step + 3 < CONV_STEPS:
                             pab_make(step + 3)
+                    if step >= CONV_STEPS:
+                        feat_turn(step, psum_conv, "conv_ps", F_BLOCK - 2)
                     feat_step(step)
                     if step < CONV_STEPS:
                         conv_finish(step)
                     if step == CONV_STEPS:
-                        nc.vector.memset(masked[1][:].bitcast(I32), 0)
+                        masked_zero(1)
                         nc.vector.reciprocal(out=rstd[:], in_=rstd[:])
                         nc.vector.tensor_mul(out=bn[:, 0:1], in0=gamma, in1=rstd[:])
                         nc.vector.tensor_mul(out=rstd[:], in0=mean, in1=bn[:, 0:1])
@@ -360,20 +370,21 @@ def tile_multiscale_gcn_pa_e_kernel(
             def graph_mask(b):
                 bank_words = slice(BANK_GROUPS * P * b, BANK_GROUPS * P * (b + 1))
                 nc.vector.tensor_copy(
-                    out=masked[b % 2][:].bitcast(I32).rearrange("p g (a c) -> p g a c", c=SLOT_STEP)[:, :, :, 0:V],
-                    in_=adj_codes[:, bank_words].bitcast(I32).rearrange("p (g a v) -> p g a v", a=SLOTS, v=V),
+                    out=masked[b % 2][:].bitcast(I32)[:, :, GAP:P],
+                    in_=adj_codes[:, bank_words].bitcast(I32).rearrange("p (c v) -> p c v", v=V),
                 )
 
             def graph_matmuls(b):
-                stat = masked[b % 2]
+                stat = masked[b % 2][:].rearrange("p c w -> p (c w)")
                 graph_ps[b] = psum_graph.tile([P, BANK_GROUPS, T], F32, name="graph_ps")
                 for gi in range(BANK_GROUPS):
                     g = BANK_GROUPS * b + gi
                     for a in range(SLOTS):
                         which, words = feat_words(SLOTS * g + a, 1)
+                        window = P * (SLOTS * gi + a) + GAP - V * a
                         nc.tensor.matmul_mx(
                             out=graph_ps[b][:, gi, :],
-                            lhsT=stat[:, gi, P * a : P * (a + 1)].bitcast(FP8X4),
+                            lhsT=stat[:, window : window + P].bitcast(FP8X4),
                             lhsT_scale=adj_scales[:, P * g : P * (g + 1)],
                             rhs=f_codes[which][:, words].bitcast(FP8X4),
                             rhs_scale=f_scales[which][:, words],
@@ -403,7 +414,7 @@ def tile_multiscale_gcn_pa_e_kernel(
                         bias=bn_slot[:, 1, g : g + 1],
                         scale=1.0,
                     )
-                nc.scalar.dma_start(out=out_view[:, BANK_GROUPS * b : BANK_GROUPS * (b + 1), :], in_=result[:])
+                nc.sync.dma_start(out=out_view[:, BANK_GROUPS * b : BANK_GROUPS * (b + 1), :], in_=result[:])
 
             def banks_started(step):
                 return [b for b in range(BANKS) if max(2 * b + 2, FLIP_END + max(b - 1, 0)) == step]
@@ -412,7 +423,7 @@ def tile_multiscale_gcn_pa_e_kernel(
                 if step + F_AHEAD < F_BLOCKS:
                     feat_load(step + F_AHEAD)
                 if step < F_BLOCKS - 1:
-                    feat_turn(step)
+                    feat_turn(step, psum_turn, "turn_ps", F_VECTOR)
                 for b in banks_started(step):
                     if b % 2 == 0:
                         adj_quantise(b // 2)

@@ -110,7 +110,7 @@ def tile_multiscale_gcn_pa_e_kernel(
         def feat_regroup(fb):
             n_vector = F_PART if fb == F_BLOCKS - 1 else F_VECTOR
             raw = f_raw[fb]
-            part1 = stage.tile([P, F_PART, T, PACK], BF16, tag="grp_scalar", bufs=3, name="part1", align_bytes=64)
+            part1 = stage.tile([P, F_PART, T, PACK], BF16, tag="grp_scalar", bufs=4, name="part1", align_bytes=64)
             if fb < FLIP_END:
                 part0 = stage.tile([P, F_PART, T, PACK], BF16, tag="grp_gpsimd", bufs=1, name="part0", align_bytes=64)
                 nc.gpsimd.tensor_scalar(
@@ -202,7 +202,7 @@ def tile_multiscale_gcn_pa_e_kernel(
             a_grp = {}
 
             def a_regroup(engine_copy, h):
-                a_grp[h] = stage.tile([P, half_cols, PACK], BF16, tag="grp_scalar", bufs=3, name="a_grp", align_bytes=64)
+                a_grp[h] = stage.tile([P, half_cols, PACK], BF16, tag="grp_scalar", bufs=4, name="a_grp", align_bytes=64)
                 engine_copy(
                     out=a_grp[h][:], in_=a_raw[:, :, half_cols * h : half_cols * (h + 1)].rearrange("p i c -> p c i")
                 )

@@ -26,7 +26,8 @@ SLOTS = 4
 GROUPS = O // SLOTS
 BANK_GROUPS = 4
 BANKS = GROUPS // BANK_GROUPS
-GAP = P - V
+CHUNK_GROUPS = 2 * BANK_GROUPS
+PLANES = SLOTS * (P + V)
 
 V_ROUND = 16
 ROUNDS = V // V_ROUND
@@ -38,6 +39,7 @@ F_AHEAD = 3
 FLIP_END = 10
 F_FIRST_TILE = F_BLOCK * FLIP_END
 F_PART = F_BLOCK // 2
+G_STEP = 1
 F_VECTOR = 2
 
 FLOPS = 2 * S * O * 512 * V * W + 2 * O * V * S * W * T
@@ -57,12 +59,7 @@ def tile_multiscale_gcn_pa_e_kernel(
         ident_f32 = keep.tile([P, P], F32, name="ident_f32")
         make_identity(nc, ident_f32[:])
 
-        masked = [
-            keep.tile([P, BANK_GROUPS * SLOTS, P], U32, name="masked%d" % i, align_bytes=64) for i in range(2)
-        ]
-
-        def masked_zero(i):
-            nc.vector.memset(masked[i][:].bitcast(I32)[:, :, 0:GAP], 0)
+        planes = [keep.tile([P, CHUNK_GROUPS, PLANES], U8, name="planes%d" % i, align_bytes=64) for i in range(2)]
 
         f_codes = [keep.tile([P, F_FIRST_TILE * T], U32, name="f_codes0", align_bytes=64)]
         f_scales = [keep.tile([P, F_FIRST_TILE * T], U8, name="f_scales0", align_bytes=64)]
@@ -109,24 +106,28 @@ def tile_multiscale_gcn_pa_e_kernel(
 
         def feat_regroup(fb):
             n_vector = F_PART if fb == F_BLOCKS - 1 else F_VECTOR
+            n_v = F_PART if fb == F_BLOCKS - 1 else 1 if fb < FLIP_END + 2 else 2
             raw = f_raw[fb]
             part1 = stage.tile([P, F_PART, T, PACK], BF16, tag="grp_scalar", bufs=4, name="part1", align_bytes=64)
             if fb < FLIP_END:
                 part0 = stage.tile([P, F_PART, T, PACK], BF16, tag="grp_gpsimd", bufs=1, name="part0", align_bytes=64)
-                nc.gpsimd.tensor_scalar(
-                    out=part0[:],
-                    in0=raw[:, 0:F_PART].rearrange("p c j t -> p c t j"),
-                    scalar1=1.0,
-                    scalar2=0.0,
-                    op0=ALU.mult,
-                    op1=ALU.add,
-                )
+                for c in range(0, F_PART, G_STEP):
+                    nc.gpsimd.tensor_scalar(
+                        out=part0[:, c : c + G_STEP],
+                        in0=raw[:, c : c + G_STEP].rearrange("p c j t -> p c t j"),
+                        scalar1=1.0,
+                        scalar2=0.0,
+                        op0=ALU.mult,
+                        op1=ALU.add,
+                    )
             else:
                 part0 = late_pool[0].tile([P, F_PART, T, PACK], BF16, tag="grp_vector", name="part0", align_bytes=64)
                 nc.vector.tensor_copy(
-                    out=part0[:, 0:n_vector].rearrange("p c (tc i) j -> p c tc j i", i=4),
-                    in_=raw[:, 0:n_vector].rearrange("p c j (tc i) -> p c tc j i", i=4),
+                    out=part0[:, 0:n_v].rearrange("p c (tc i) j -> p c tc j i", i=4),
+                    in_=raw[:, 0:n_v].rearrange("p c j (tc i) -> p c tc j i", i=4),
                 )
+                for c in range(n_v, n_vector):
+                    regroup_on_scalar(part0[:, c], raw[:, c])
             n_scalar = F_PART - 2 if CONV_STEPS <= fb < FLIP_END else F_PART
             for c in range(n_scalar):
                 regroup_on_scalar(part1[:, c], raw[:, F_PART + c])
@@ -197,7 +198,6 @@ def tile_multiscale_gcn_pa_e_kernel(
             nc.sync.dma_start(out=w_words[:, S // 2 : S].bitcast(I32), in_=w_view[:, S // 2 : S])
             feat_load(1)
             feat_load(2)
-            masked_zero(0)
 
             a_grp = {}
 
@@ -253,6 +253,9 @@ def tile_multiscale_gcn_pa_e_kernel(
                 nc.scalar.sqrt(out=rstd[:], in_=rstd[:])
                 for step in range(1, 4):
                     pab_make(step)
+                for i in range(2):
+                    nc.vector.memset(planes[i][:].bitcast(I32), 0)
+                nc.vector.memset(adj_scales[:].bitcast(I32), 0)
                 a_regroup(nc.vector.tensor_copy, 1)
                 a_quantise(1)
                 adj_words = (
@@ -317,21 +320,20 @@ def tile_multiscale_gcn_pa_e_kernel(
                             x_tiles[step // (S // S_STEP)] = conv.tile(
                                 [P, V_ROUND, S, W], BF16, tag="x", bufs=2, name="x"
                             )
-                        conv_matmuls(step)
                         if 1 <= step and step + 3 < CONV_STEPS:
                             pab_make(step + 3)
+                        conv_matmuls(step)
                     if step >= CONV_STEPS:
                         feat_turn(step, psum_conv, "conv_ps", F_BLOCK - 2)
                     feat_step(step)
                     if step < CONV_STEPS:
                         conv_finish(step)
                     if step == CONV_STEPS:
-                        masked_zero(1)
                         nc.vector.reciprocal(out=rstd[:], in_=rstd[:])
                         nc.vector.tensor_mul(out=bn[:, 0:1], in0=gamma, in1=rstd[:])
                         nc.vector.tensor_mul(out=rstd[:], in0=mean, in1=bn[:, 0:1])
                         nc.vector.tensor_sub(out=bn[:, 1:2], in0=beta, in1=rstd[:])
-                    n_vector = max(0, step - CONV_STEPS + 1)
+                    n_vector = 2 if step >= CONV_STEPS else 0
                     for i, pair in enumerate(pairs_of_step(step)):
                         flip_pair(pair, nc.vector.tensor_copy if i >= 4 - n_vector else nc.scalar.copy)
 
@@ -367,25 +369,24 @@ def tile_multiscale_gcn_pa_e_kernel(
                     in_=adj[:, o_step * c : o_step * (c + 1)].rearrange("p o v j -> p (o v j)"),
                 )
 
-            def graph_mask(b):
-                bank_words = slice(BANK_GROUPS * P * b, BANK_GROUPS * P * (b + 1))
+            def planes_fill(c):
+                columns = slice(CHUNK_GROUPS * P * c, CHUNK_GROUPS * P * (c + 1))
                 nc.vector.tensor_copy(
-                    out=masked[b % 2][:].bitcast(I32)[:, :, GAP:P],
-                    in_=adj_codes[:, bank_words].bitcast(I32).rearrange("p (c v) -> p c v", v=V),
+                    out=planes[c % 2][:].bitcast(I32).rearrange("p g (a y) -> p g a y", a=SLOTS)[:, :, :, 0:W8],
+                    in_=adj_scales[:, columns].bitcast(I32).rearrange("p (g a v) -> p g a v", a=SLOTS, v=W8),
                 )
 
             def graph_matmuls(b):
-                stat = masked[b % 2][:].rearrange("p c w -> p (c w)")
                 graph_ps[b] = psum_graph.tile([P, BANK_GROUPS, T], F32, name="graph_ps")
                 for gi in range(BANK_GROUPS):
                     g = BANK_GROUPS * b + gi
                     for a in range(SLOTS):
                         which, words = feat_words(SLOTS * g + a, 1)
-                        window = P * (SLOTS * gi + a) + GAP - V * a
+                        c, gc = divmod(g, CHUNK_GROUPS)
                         nc.tensor.matmul_mx(
                             out=graph_ps[b][:, gi, :],
-                            lhsT=stat[:, window : window + P].bitcast(FP8X4),
-                            lhsT_scale=adj_scales[:, P * g : P * (g + 1)],
+                            lhsT=adj_codes[:, P * g : P * (g + 1)].bitcast(FP8X4),
+                            lhsT_scale=planes[c % 2][:, gc, P * a : P * (a + 1)],
                             rhs=f_codes[which][:, words].bitcast(FP8X4),
                             rhs_scale=f_scales[which][:, words],
                             start=(a == 0),
@@ -394,7 +395,7 @@ def tile_multiscale_gcn_pa_e_kernel(
 
             def graph_finish(b):
                 scaled = late.tile([P, BANK_GROUPS, T], F32, name="scaled")
-                result = late.tile([P, BANK_GROUPS, T], F32, name="result")
+                result = late.tile([P, BANK_GROUPS, T], F32, bufs=3, name="result")
                 for gi in range(BANK_GROUPS):
                     g = BANK_GROUPS * b + gi
                     nc.vector.scalar_tensor_tensor(
@@ -427,7 +428,7 @@ def tile_multiscale_gcn_pa_e_kernel(
                 for b in banks_started(step):
                     if b % 2 == 0:
                         adj_quantise(b // 2)
-                    graph_mask(b)
+                        planes_fill(b // 2)
                 if step <= F_BLOCKS:
                     feat_quantise(step - 1)
                 for b in banks_started(step):

@@ -39,7 +39,6 @@ F_AHEAD = 3
 FLIP_END = 10
 F_FIRST_TILE = F_BLOCK * FLIP_END
 F_PART = F_BLOCK // 2
-G_STEP = 1
 F_VECTOR = 2
 
 FLOPS = 2 * S * O * 512 * V * W + 2 * O * V * S * W * T
@@ -111,15 +110,14 @@ def tile_multiscale_gcn_pa_e_kernel(
             part1 = stage.tile([P, F_PART, T, PACK], BF16, tag="grp_scalar", bufs=4, name="part1", align_bytes=64)
             if fb < FLIP_END:
                 part0 = stage.tile([P, F_PART, T, PACK], BF16, tag="grp_gpsimd", bufs=1, name="part0", align_bytes=64)
-                for c in range(0, F_PART, G_STEP):
-                    nc.gpsimd.tensor_scalar(
-                        out=part0[:, c : c + G_STEP],
-                        in0=raw[:, c : c + G_STEP].rearrange("p c j t -> p c t j"),
-                        scalar1=1.0,
-                        scalar2=0.0,
-                        op0=ALU.mult,
-                        op1=ALU.add,
-                    )
+                nc.gpsimd.tensor_scalar(
+                    out=part0[:],
+                    in0=raw[:, 0:F_PART].rearrange("p c j t -> p c t j"),
+                    scalar1=1.0,
+                    scalar2=0.0,
+                    op0=ALU.mult,
+                    op1=ALU.add,
+                )
             else:
                 part0 = late_pool[0].tile([P, F_PART, T, PACK], BF16, tag="grp_vector", name="part0", align_bytes=64)
                 nc.vector.tensor_copy(

@@ -168,12 +168,16 @@ def tile_multiscale_gcn_pa_e_kernel(
             prm = keep.tile([P, S + 4], F32, name="prm")
             bn = keep.tile([P, 2], F32, name="bn")
             rstd = keep.tile([P, 1], F32, name="rstd")
+            bn_slot = keep.tile([P, 2, GROUPS], F32, name="bn_slot")
 
             warm = keep.tile([P, 1], F32, name="warm")
             nc.vector.memset(prm_rows[:], 0.0)
             nc.vector.memset(rstd[:], 1.0)
             nc.vector.memset(w_scales[:].bitcast(I32), 0)
             nc.vector.memset(pa_rows[P // 2 : P, :], 0.0)
+            for i in range(2):
+                nc.gpsimd.memset(planes[i][:].bitcast(F32), 0.0)
+            nc.gpsimd.memset(adj_scales[:].bitcast(F32), 0.0)
             nc.scalar.dma_start(out=prm_rows[0:S, :], in_=ada_b)
             for r, vec in enumerate((bn_gamma, bn_beta, bn_mean, bn_var)):
                 nc.scalar.dma_start(out=prm_rows[S + r : S + r + 1, :], in_=vec.unsqueeze(0))
@@ -227,7 +231,10 @@ def tile_multiscale_gcn_pa_e_kernel(
                     pab[step] = conv.tile([P, S_STEP, n_cols], BF16, tag="pab", bufs=4, name="pab")
                     pab_words = pab[step][:].rearrange("p s c -> p (s c)").bitcast(F32)
                     for half in range(2):
-                        pab_ps = psum_pab.tile([P, 4, P], F32, name="pab_ps")
+                        if step < 4 and half == 1:
+                            pab_ps = psum_flip.tile([P, 4, P], F32, tag="flip_ps", name="pab_ps")
+                        else:
+                            pab_ps = psum_pab.tile([P, 4, P], F32, tag="pab_ps", name="pab_ps")
                         for k in range(4):
                             c = 4 * (S_STEP * quarter + 2 * half + k // 2) + 2 * r + k % 2
                             nc.tensor.transpose(
@@ -251,11 +258,11 @@ def tile_multiscale_gcn_pa_e_kernel(
                 nc.scalar.sqrt(out=rstd[:], in_=rstd[:])
                 for step in range(1, 4):
                     pab_make(step)
-                for i in range(2):
-                    nc.vector.memset(planes[i][:].bitcast(I32), 0)
-                nc.vector.memset(adj_scales[:].bitcast(I32), 0)
+                nc.vector.reciprocal(out=rstd[:], in_=rstd[:])
+                nc.vector.tensor_mul(out=bn[:, 0:1], in0=gamma, in1=rstd[:])
+                nc.vector.tensor_mul(out=rstd[:], in0=mean, in1=bn[:, 0:1])
+                nc.vector.tensor_sub(out=bn[:, 1:2], in0=beta, in1=rstd[:])
                 a_regroup(nc.vector.tensor_copy, 1)
-                a_quantise(1)
                 adj_words = (
                     adj[:]
                     .rearrange("p o v j -> p (o v j)")
@@ -291,9 +298,9 @@ def tile_multiscale_gcn_pa_e_kernel(
                             op1=ALU.mult,
                         )
 
-                def flip_pair(pair, engine_copy):
+                def flip_pair(pair, engine_copy, pool=psum_flip, tag="flip_ps"):
                     r, v_local = divmod(2 * pair, V_ROUND)
-                    flip_ps = psum_flip.tile([P, 2, 2, O], F32, name="flip_ps")
+                    flip_ps = pool.tile([P, 2, 2, O], F32, tag=tag, name="flip_ps")
                     for dv in range(2):
                         for u in range(2):
                             nc.tensor.transpose(
@@ -326,20 +333,24 @@ def tile_multiscale_gcn_pa_e_kernel(
                     feat_step(step)
                     if step < CONV_STEPS:
                         conv_finish(step)
-                    if step == CONV_STEPS:
-                        nc.vector.reciprocal(out=rstd[:], in_=rstd[:])
-                        nc.vector.tensor_mul(out=bn[:, 0:1], in0=gamma, in1=rstd[:])
-                        nc.vector.tensor_mul(out=rstd[:], in0=mean, in1=bn[:, 0:1])
-                        nc.vector.tensor_sub(out=bn[:, 1:2], in0=beta, in1=rstd[:])
-                    n_vector = 2 if step >= CONV_STEPS else 0
+                    if step == 0:
+                        a_quantise(1)
+                    if step == FLIP_END - 1:
+                        bn_ps = psum_conv.tile([P, 2, P], F32, tag="conv_ps", name="bn_ps")
+                        for c in range(2):
+                            nc.tensor.transpose(bn_ps[:, c, :], bn[:, c : c + 1].to_broadcast([P, P]), ident_f32[:])
+                        for a in range(SLOTS):
+                            rows = slice(V * a, V * a + V)
+                            nc.vector.tensor_copy(out=bn_slot[rows], in_=bn_ps[rows, :, a:P:SLOTS])
                     for i, pair in enumerate(pairs_of_step(step)):
-                        flip_pair(pair, nc.vector.tensor_copy if i >= 4 - n_vector else nc.scalar.copy)
+                        if step >= CONV_STEPS and i % 2 == 0:
+                            flip_pair(pair, nc.vector.tensor_copy, psum_conv, "conv_ps")
+                        else:
+                            flip_pair(pair, nc.scalar.copy)
 
         with tc.tile_pool(name="late", bufs=2, reuse_waits="tile") as late, tc.psum_pool(
             name="psum_graph", bufs=4
-        ) as psum_graph, tc.psum_pool(name="psum_bn", bufs=1) as psum_bn, tc.psum_pool(
-            name="psum_turn", bufs=2
-        ) as psum_turn:
+        ) as psum_graph, tc.psum_pool(name="psum_turn", bufs=3) as psum_turn:
             late_pool.append(late)
             late_pool.append(psum_turn)
             f_codes.append(late.tile([P, (O - F_FIRST_TILE) * T], U32, bufs=1, name="f_codes1", align_bytes=64))
@@ -347,14 +358,6 @@ def tile_multiscale_gcn_pa_e_kernel(
             out_view = out.rearrange("n (g a) v t -> (n a v) g t", a=SLOTS)
             res_sb = late.tile([P, GROUPS, T], BF16, bufs=1, name="res_sb")
             nc.sync.dma_start(out=res_sb[:], in_=res.rearrange("n (g a) v t -> (n a v) g t", a=SLOTS))
-
-            bn_ps = psum_bn.tile([P, 2, P], F32, name="bn_ps")
-            for c in range(2):
-                nc.tensor.transpose(bn_ps[:, c, :], bn[:, c : c + 1].to_broadcast([P, P]), ident_f32[:])
-            bn_slot = keep.tile([P, 2, GROUPS], F32, name="bn_slot")
-            for a in range(SLOTS):
-                rows = slice(V * a, V * a + V)
-                nc.vector.tensor_copy(out=bn_slot[rows], in_=bn_ps[rows, :, a:P:SLOTS])
 
             graph_ps = {}
 

@@ -105,7 +105,7 @@ def tile_multiscale_gcn_pa_e_kernel(
 
         def feat_regroup(fb):
             n_vector = F_PART if fb == F_BLOCKS - 1 else F_VECTOR
-            n_v = F_PART if fb == F_BLOCKS - 1 else 1 if fb < FLIP_END + 2 else 2
+            n_v = F_PART if fb == F_BLOCKS - 1 else 1 if fb < FLIP_END + 1 else 2
             raw = f_raw[fb]
             part1 = stage.tile([P, F_PART, T, PACK], BF16, tag="grp_scalar", bufs=4, name="part1", align_bytes=64)
             if fb < FLIP_END:
@@ -343,7 +343,7 @@ def tile_multiscale_gcn_pa_e_kernel(
                             rows = slice(V * a, V * a + V)
                             nc.vector.tensor_copy(out=bn_slot[rows], in_=bn_ps[rows, :, a:P:SLOTS])
                     for i, pair in enumerate(pairs_of_step(step)):
-                        if step >= CONV_STEPS and i % 2 == 0:
+                        if step >= CONV_STEPS and i in (0, 2, 3):
                             flip_pair(pair, nc.vector.tensor_copy, psum_conv, "conv_ps")
                         else:
                             flip_pair(pair, nc.scalar.copy)

from contextlib import ExitStack

import concourse.mybir as mybir
from concourse.masks import make_identity

F32 = mybir.dt.float32
BF16 = mybir.dt.bfloat16
U32 = mybir.dt.uint32
I32 = mybir.dt.int32
U8 = mybir.dt.uint8
FP8X4 = mybir.dt.float8_e4m3fn_x4
ALU = mybir.AluOpType
ACT = mybir.ActivationFunctionType

P = 128
PACK = 4
S = 16
O = 128
V = 32
W = 32
W8 = W // PACK
T = 128
EPS = 1e-5

SLOTS = 4
GROUPS = O // SLOTS
BANK_GROUPS = 4
BANKS = GROUPS // BANK_GROUPS
CHUNK_GROUPS = 2 * BANK_GROUPS
PLANES = SLOTS * (P + V)

V_ROUND = 16
ROUNDS = V // V_ROUND
S_STEP = 4
CONV_STEPS = ROUNDS * S // S_STEP
F_BLOCK = 8
F_BLOCKS = O // F_BLOCK
F_AHEAD = 3
FLIP_END = 10
F_FIRST_TILE = F_BLOCK * FLIP_END
F_PART = F_BLOCK // 2
F_VECTOR = 2

FLOPS = 2 * S * O * 512 * V * W + 2 * O * V * S * W * T


def tile_multiscale_gcn_pa_e_kernel(
    tc, ada_A, ada_w_words, ada_w_scales, ada_b, PA, feat, bn_gamma, bn_beta, bn_mean, bn_var, res, out
):
    nc = tc.nc
    with ExitStack() as ctx:
        ctx.enter_context(tc.manual_schedule())
        keep = ctx.enter_context(tc.tile_pool(name="keep", bufs=1))
        stage = ctx.enter_context(tc.tile_pool(name="stage", bufs=3))

        ident_bf = keep.tile([P, P], BF16, name="ident_bf")
        make_identity(nc, ident_bf[:])
        ident_f32 = keep.tile([P, P], F32, name="ident_f32")
        make_identity(nc, ident_f32[:])

        planes = [keep.tile([P, CHUNK_GROUPS, PLANES], U8, name="planes%d" % i, align_bytes=64) for i in range(2)]

        f_codes = [keep.tile([P, F_FIRST_TILE * T], U32, name="f_codes0", align_bytes=64)]
        f_scales = [keep.tile([P, F_FIRST_TILE * T], U8, name="f_scales0", align_bytes=64)]
        adj_codes = keep.tile([P, O * V], U32, name="adj_codes", align_bytes=64)
        adj_scales = keep.tile([P, O * V], U8, name="adj_scales", align_bytes=64)
        adj = keep.tile([P, O, V, PACK], BF16, name="adj", align_bytes=64)

        def feat_words(o, n):
            which = 0 if o < F_FIRST_TILE else 1
            first = o - which * F_FIRST_TILE
            return which, slice(T * first, T * (first + n))

        f_raw = {}
        f_grp = {}
        late_pool = []

        def feat_load(fb):
            f_raw[fb] = stage.tile([P, F_BLOCK, PACK, T], BF16, tag="raw", bufs=F_AHEAD + 1, name="f_raw", align_bytes=64)
            for c in range(F_BLOCK):
                nc.sync.dma_start(
                    out=f_raw[fb][:, c].rearrange("p j t -> p (j t)"),
                    in_=feat[:, 0, F_BLOCK * fb + c].rearrange("s (w8 j) t -> s w8 (j t)", j=PACK),
                )

        def regroup_on_scalar(dst, src):
            nc.scalar.copy(
                out=dst.rearrange("p (tc i) j -> p tc j i", i=4), in_=src.rearrange("p j (tc i) -> p tc j i", i=4)
            )

        f_turn = {}

        def feat_turn(fb, pool, tag, first):
            f_turn[fb] = pool.tile([P, T * PACK], F32, tag=tag, name="turn_ps")
            for i in range(2):
                nc.tensor.matmul(
                    out=f_turn[fb][:, T * PACK // 2 * i : T * PACK // 2 * (i + 1)]
                    .bitcast(BF16)
                    .rearrange("p (t j) -> p t j", j=PACK),
                    lhsT=ident_bf[:],
                    rhs=f_raw[fb][:, first + i].rearrange("p j t -> p t j"),
                    start=True,
                    stop=True,
                )

        def feat_regroup(fb):
            n_vector = F_PART if fb == F_BLOCKS - 1 else F_VECTOR
            n_v = F_PART if fb == F_BLOCKS - 1 else 1 if fb < FLIP_END + 1 else 2
            raw = f_raw[fb]
            part1 = stage.tile([P, F_PART, T, PACK], BF16, tag="grp_scalar", bufs=4, name="part1", align_bytes=64)
            if fb < FLIP_END:
                part0 = stage.tile([P, F_PART, T, PACK], BF16, tag="grp_gpsimd", bufs=1, name="part0", align_bytes=64)
                nc.gpsimd.tensor_scalar(
                    out=part0[:],
                    in0=raw[:, 0:F_PART].rearrange("p c j t -> p c t j"),
                    scalar1=1.0,
                    scalar2=0.0,
                    op0=ALU.mult,
                    op1=ALU.add,
                )
            else:
                part0 = late_pool[0].tile([P, F_PART, T, PACK], BF16, tag="grp_vector", name="part0", align_bytes=64)
                nc.vector.tensor_copy(
                    out=part0[:, 0:n_v].rearrange("p c (tc i) j -> p c tc j i", i=4),
                    in_=raw[:, 0:n_v].rearrange("p c j (tc i) -> p c tc j i", i=4),
                )
                for c in range(n_v, n_vector):
                    regroup_on_scalar(part0[:, c], raw[:, c])
            n_scalar = F_PART - 2 if CONV_STEPS <= fb < FLIP_END else F_PART
            for c in range(n_scalar):
                regroup_on_scalar(part1[:, c], raw[:, F_PART + c])
            if n_scalar < F_PART:
                nc.scalar.copy(
                    out=part1[:, n_scalar:F_PART].rearrange("p c t j -> p (c t j)").bitcast(F32), in_=f_turn[fb][:]
                )
            if fb >= FLIP_END and n_vector < F_PART:
                nc.scalar.copy(
                    out=part0[:, n_vector:F_PART].rearrange("p c t j -> p (c t j)").bitcast(F32), in_=f_turn[fb][:]
                )
            f_grp[fb] = (part0, part1)

        def feat_quantise(fb):
            for part in (1, 0):
                which, words = feat_words(F_BLOCK * fb + F_PART * part, F_PART)
                nc.vector.quantize_mx(
                    out=f_codes[which][:, words].bitcast(FP8X4),
                    scales=f_scales[which][:, words],
                    in_=f_grp[fb][part][:].rearrange("p c t j -> p (c t j)"),
                )

        def feat_step(step):
            if step + F_AHEAD < F_BLOCKS:
                feat_load(step + F_AHEAD)
            if 1 <= step <= F_BLOCKS:
                feat_quantise(step - 1)
            if step < F_BLOCKS:
                feat_regroup(step)

        with tc.tile_pool(name="conv", bufs=1) as conv:
            x_tiles = {}
            w_words = conv.tile([P, S, P], U32, name="w_words", align_bytes=64)
            w_scales = conv.tile([P, S, P], U8, name="w_scales", align_bytes=64)
            a_codes = conv.tile([P, V * W], U32, name="a_codes", align_bytes=64)
            a_scales = conv.tile([P, V * W], U8, name="a_scales", align_bytes=64)
            prm_rows = conv.tile([P, P], BF16, name="prm_rows")
            pa_rows = conv.tile([P, 2 * P], BF16, name="pa_rows")
            pa_cols = conv.tile([P, P // 2], F32, name="pa_cols")
            prm = keep.tile([P, S + 4], F32, name="prm")
            bn = keep.tile([P, 2], F32, name="bn")
            rstd = keep.tile([P, 1], F32, name="rstd")
            bn_slot = keep.tile([P, 2, GROUPS], F32, name="bn_slot")

            warm = keep.tile([P, 1], F32, name="warm")
            nc.vector.memset(prm_rows[:], 0.0)
            nc.vector.memset(rstd[:], 1.0)
            nc.vector.memset(w_scales[:].bitcast(I32), 0)
            nc.vector.memset(pa_rows[P // 2 : P, :], 0.0)
            for i in range(2):
                nc.gpsimd.memset(planes[i][:].bitcast(F32), 0.0)
            nc.gpsimd.memset(adj_scales[:].bitcast(F32), 0.0)
            nc.scalar.dma_start(out=prm_rows[0:S, :], in_=ada_b)
            for r, vec in enumerate((bn_gamma, bn_beta, bn_mean, bn_var)):
                nc.scalar.dma_start(out=prm_rows[S + r : S + r + 1, :], in_=vec.unsqueeze(0))
            nc.scalar.sqrt(out=warm[:], in_=rstd[:])
            a_raw = stage.tile([P, PACK, V * W], BF16, tag="raw", bufs=F_AHEAD + 1, name="a_raw", align_bytes=64)
            a_view = ada_A.rearrange("n (p i) v w -> p (n i) (v w)", i=PACK)
            half_cols = V * W // 2
            w_view = ada_w_words.rearrange("g p n t -> p g (n t)").bitcast(I32)
            nc.sync.dma_start(out=pa_rows[0 : P // 2, :], in_=PA.rearrange("s (vh vl) w -> (s vh) (vl w)", vl=8))
            nc.sync.dma_start(out=a_raw[:, :, 0:half_cols], in_=a_view[:, :, 0:half_cols])
            for quad in range(4):
                nc.sync.dma_start(
                    out=w_scales[32 * quad : 32 * quad + 4].bitcast(I32),
                    in_=ada_w_scales[:, 4 * quad : 4 * quad + 4, :].rearrange("g r n -> r g n").bitcast(I32),
                )
            nc.sync.dma_start(out=w_words[:, 0:S_STEP].bitcast(I32), in_=w_view[:, 0:S_STEP])
            nc.sync.dma_start(out=a_raw[:, :, half_cols : 2 * half_cols], in_=a_view[:, :, half_cols : 2 * half_cols])
            feat_load(0)
            nc.sync.dma_start(out=w_words[:, S_STEP : S // 2].bitcast(I32), in_=w_view[:, S_STEP : S // 2])
            nc.sync.dma_start(out=w_words[:, S // 2 : S].bitcast(I32), in_=w_view[:, S // 2 : S])
            feat_load(1)
            feat_load(2)

            a_grp = {}

            def a_regroup(engine_copy, h):
                a_grp[h] = stage.tile([P, half_cols, PACK], BF16, tag="grp_scalar", bufs=4, name="a_grp", align_bytes=64)
                engine_copy(
                    out=a_grp[h][:], in_=a_raw[:, :, half_cols * h : half_cols * (h + 1)].rearrange("p i c -> p c i")
                )

            def a_quantise(h):
                cols = slice(half_cols * h, half_cols * (h + 1))
                nc.vector.quantize_mx(
                    out=a_codes[:, cols].bitcast(FP8X4),
                    scales=a_scales[:, cols],
                    in_=a_grp[h][:].rearrange("p c i -> p (c i)"),
                )

            gamma, beta, mean, var = [prm[:, S + r : S + r + 1] for r in range(4)]

            with tc.psum_pool(name="psum_conv", bufs=4) as psum_conv, tc.psum_pool(
                name="psum_flip", bufs=2
            ) as psum_flip, tc.psum_pool(name="psum_pab", bufs=2) as psum_pab:
                n_cols = V_ROUND * W
                conv_ps = {}
                pab = {}

                def pab_make(step):
                    r, quarter = divmod(step, S // S_STEP)
                    pab[step] = conv.tile([P, S_STEP, n_cols], BF16, tag="pab", bufs=4, name="pab")
                    pab_words = pab[step][:].rearrange("p s c -> p (s c)").bitcast(F32)
                    for half in range(2):
                        if step < 4 and half == 1:
                            pab_ps = psum_flip.tile([P, 4, P], F32, tag="flip_ps", name="pab_ps")
                        else:
                            pab_ps = psum_pab.tile([P, 4, P], F32, tag="pab_ps", name="pab_ps")
                        for k in range(4):
                            c = 4 * (S_STEP * quarter + 2 * half + k // 2) + 2 * r + k % 2
                            nc.tensor.transpose(
                                pab_ps[:, k, :], pa_cols[:, c : c + 1].to_broadcast([P, P]), ident_f32[:]
                            )
                        nc.scalar.copy(
                            out=pab_words[:, 4 * P * half : 4 * P * (half + 1)],
                            in_=pab_ps[:].rearrange("p k n -> p (k n)"),
                        )

                pa_ps = psum_flip.tile([P, P], F32, tag="flip_ps", name="pa_ps")
                nc.tensor.transpose(pa_ps[:], pa_rows[:].bitcast(F32), ident_f32[:])
                nc.vector.tensor_copy(out=pa_cols[:], in_=pa_ps[:, 0 : P // 2])
                pab_make(0)
                a_regroup(nc.vector.tensor_copy, 0)
                a_quantise(0)
                prm_ps = psum_flip.tile([P, P], BF16, tag="flip_ps", name="prm_ps")
                nc.tensor.transpose(prm_ps[:], prm_rows[:], ident_bf[:])
                nc.vector.tensor_copy(out=prm[:], in_=prm_ps[:, 0 : S + 4])
                nc.vector.tensor_scalar_add(out=rstd[:], in0=var, scalar1=EPS)
                nc.scalar.sqrt(out=rstd[:], in_=rstd[:])
                for step in range(1, 4):
                    pab_make(step)
                nc.vector.reciprocal(out=rstd[:], in_=rstd[:])
                nc.vector.tensor_mul(out=bn[:, 0:1], in0=gamma, in1=rstd[:])
                nc.vector.tensor_mul(out=rstd[:], in0=mean, in1=bn[:, 0:1])
                nc.vector.tensor_sub(out=bn[:, 1:2], in0=beta, in1=rstd[:])
                a_regroup(nc.vector.tensor_copy, 1)
                adj_words = (
                    adj[:]
                    .rearrange("p o v j -> p (o v j)")
                    .bitcast(F32)
                    .rearrange("p (o v u) -> p o v u", v=V, u=2)
                )

                def conv_matmuls(step):
                    r, quarter = divmod(step, S // S_STEP)
                    cols = slice(n_cols * r, n_cols * (r + 1))
                    for s in range(S_STEP * quarter, S_STEP * (quarter + 1)):
                        conv_ps[s] = psum_conv.tile([P, n_cols], F32, name="conv_ps")
                        nc.tensor.matmul_mx(
                            out=conv_ps[s][:],
                            lhsT=w_words[:, s, :].bitcast(FP8X4),
                            lhsT_scale=w_scales[:, s, :],
                            rhs=a_codes[:, cols].bitcast(FP8X4),
                            rhs_scale=a_scales[:, cols],
                            start=True,
                            stop=True,
                        )

                def conv_finish(step):
                    r, quarter = divmod(step, S // S_STEP)
                    for i in range(S_STEP):
                        s = S_STEP * quarter + i
                        nc.vector.scalar_tensor_tensor(
                            out=x_tiles[r][:, :, s, :],
                            in0=conv_ps[s][:].rearrange("p (v w) -> p v w", w=W),
                            scalar=prm[:, s : s + 1],
                            in1=pab[step][:, i, :].rearrange("p (v w) -> p v w", w=W),
                            op0=ALU.add,
                            op1=ALU.mult,
                        )

                def flip_pair(pair, engine_copy, pool=psum_flip, tag="flip_ps"):
                    r, v_local = divmod(2 * pair, V_ROUND)
                    flip_ps = pool.tile([P, 2, 2, O], F32, tag=tag, name="flip_ps")
                    for dv in range(2):
                        for u in range(2):
                            nc.tensor.transpose(
                                flip_ps[:, dv, u, :],
                                x_tiles[r][:, v_local + dv].rearrange("p s w -> p (s w)").bitcast(F32)[:, u : S * W // 2 : 2],
                                ident_f32[:],
                            )
                    engine_copy(
                        out=adj_words[:, :, 2 * pair : 2 * pair + 2, :], in_=flip_ps[:].rearrange("p v u o -> p o v u")
                    )

                def pairs_of_step(step):
                    if 4 <= step < 8:
                        return range(2 * (step - 4), 2 * (step - 3))
                    if step >= 8:
                        return range(8 + 4 * (step - 8), 8 + 4 * (step - 7))
                    return range(0)

                for step in range(FLIP_END):
                    if step < CONV_STEPS:
                        if step % (S // S_STEP) == 0:
                            x_tiles[step // (S // S_STEP)] = conv.tile(
                                [P, V_ROUND, S, W], BF16, tag="x", bufs=2, name="x"
                            )
                        if 1 <= step and step + 3 < CONV_STEPS:
                            pab_make(step + 3)
                        conv_matmuls(step)
                    if step >= CONV_STEPS:
                        feat_turn(step, psum_conv, "conv_ps", F_BLOCK - 2)
                    feat_step(step)
                    if step < CONV_STEPS:
                        conv_finish(step)
                    if step == 0:
                        a_quantise(1)
                    if step == FLIP_END - 1:
                        bn_ps = psum_conv.tile([P, 2, P], F32, tag="conv_ps", name="bn_ps")
                        for c in range(2):
                            nc.tensor.transpose(bn_ps[:, c, :], bn[:, c : c + 1].to_broadcast([P, P]), ident_f32[:])
                        for a in range(SLOTS):
                            rows = slice(V * a, V * a + V)
                            nc.vector.tensor_copy(out=bn_slot[rows], in_=bn_ps[rows, :, a:P:SLOTS])
                    for i, pair in enumerate(pairs_of_step(step)):
                        if step >= CONV_STEPS and i in (0, 2, 3):
                            flip_pair(pair, nc.vector.tensor_copy, psum_conv, "conv_ps")
                        else:
                            flip_pair(pair, nc.scalar.copy)

        with tc.tile_pool(name="late", bufs=2, reuse_waits="tile") as late, tc.psum_pool(
            name="psum_graph", bufs=4
        ) as psum_graph, tc.psum_pool(name="psum_turn", bufs=3) as psum_turn:
            late_pool.append(late)
            late_pool.append(psum_turn)
            f_codes.append(late.tile([P, (O - F_FIRST_TILE) * T], U32, bufs=1, name="f_codes1", align_bytes=64))
            f_scales.append(late.tile([P, (O - F_FIRST_TILE) * T], U8, bufs=1, name="f_scales1", align_bytes=64))
            out_view = out.rearrange("n (g a) v t -> (n a v) g t", a=SLOTS)
            res_sb = late.tile([P, GROUPS, T], BF16, bufs=1, name="res_sb")
            nc.sync.dma_start(out=res_sb[:], in_=res.rearrange("n (g a) v t -> (n a v) g t", a=SLOTS))

            graph_ps = {}

            def adj_quantise(c):
                o_step = 2 * BANK_GROUPS * SLOTS
                words = slice(V * o_step * c, V * o_step * (c + 1))
                nc.vector.quantize_mx(
                    out=adj_codes[:, words].bitcast(FP8X4),
                    scales=adj_scales[:, words],
                    in_=adj[:, o_step * c : o_step * (c + 1)].rearrange("p o v j -> p (o v j)"),
                )

            def planes_fill(c):
                columns = slice(CHUNK_GROUPS * P * c, CHUNK_GROUPS * P * (c + 1))
                nc.vector.tensor_copy(
                    out=planes[c % 2][:].bitcast(I32).rearrange("p g (a y) -> p g a y", a=SLOTS)[:, :, :, 0:W8],
                    in_=adj_scales[:, columns].bitcast(I32).rearrange("p (g a v) -> p g a v", a=SLOTS, v=W8),
                )

            def graph_matmuls(b):
                graph_ps[b] = psum_graph.tile([P, BANK_GROUPS, T], F32, name="graph_ps")
                for gi in range(BANK_GROUPS):
                    g = BANK_GROUPS * b + gi
                    for a in range(SLOTS):
                        which, words = feat_words(SLOTS * g + a, 1)
                        c, gc = divmod(g, CHUNK_GROUPS)
                        nc.tensor.matmul_mx(
                            out=graph_ps[b][:, gi, :],
                            lhsT=adj_codes[:, P * g : P * (g + 1)].bitcast(FP8X4),
                            lhsT_scale=planes[c % 2][:, gc, P * a : P * (a + 1)],
                            rhs=f_codes[which][:, words].bitcast(FP8X4),
                            rhs_scale=f_scales[which][:, words],
                            start=(a == 0),
                            stop=(a == SLOTS - 1),
                        )

            def graph_finish(b):
                scaled = late.tile([P, BANK_GROUPS, T], F32, name="scaled")
                result = late.tile([P, BANK_GROUPS, T], F32, bufs=3, name="result")
                for gi in range(BANK_GROUPS):
                    g = BANK_GROUPS * b + gi
                    nc.vector.scalar_tensor_tensor(
                        out=scaled[:, gi, :],
                        in0=graph_ps[b][:, gi, :],
                        scalar=bn_slot[:, 0, g : g + 1],
                        in1=res_sb[:, g, :],
                        op0=ALU.mult,
                        op1=ALU.add,
                    )
                for gi in range(BANK_GROUPS):
                    g = BANK_GROUPS * b + gi
                    nc.scalar.activation(
                        out=result[:, gi, :],
                        in_=scaled[:, gi, :],
                        func=ACT.Relu,
                        bias=bn_slot[:, 1, g : g + 1],
                        scale=1.0,
                    )
                nc.sync.dma_start(out=out_view[:, BANK_GROUPS * b : BANK_GROUPS * (b + 1), :], in_=result[:])

            def banks_started(step):
                return [b for b in range(BANKS) if max(2 * b + 2, FLIP_END + max(b - 1, 0)) == step]

            for step in range(FLIP_END, F_BLOCKS + 2):
                if step + F_AHEAD < F_BLOCKS:
                    feat_load(step + F_AHEAD)
                if step < F_BLOCKS - 1:
                    feat_turn(step, psum_turn, "turn_ps", F_VECTOR)
                for b in banks_started(step):
                    if b % 2 == 0:
                        adj_quantise(b // 2)
                        planes_fill(b // 2)
                if step <= F_BLOCKS:
                    feat_quantise(step - 1)
                for b in banks_started(step):
                    graph_matmuls(b)
                if step < F_BLOCKS:
                    feat_regroup(step)
                for b in banks_started(step - 1):
                    graph_finish(b)
